import numpy as np
import ml_dtypes


def mxq(x, axis, fmt="e4m3"):
    dtype, down = {"e4m3": (ml_dtypes.float8_e4m3fn, 7), "e5m2": (ml_dtypes.float8_e5m2, 14)}[fmt]
    v = np.moveaxis(np.asarray(x, np.float32).astype(ml_dtypes.bfloat16).astype(np.float64), axis, -1)
    blocks = v.reshape(v.shape[:-1] + (-1, 32))
    amax = np.abs(blocks).max(-1, keepdims=True)
    byte = np.maximum(np.where(amax > 0, np.frexp(amax)[1] - 1 + 127, 0) - down, 1)
    scale = np.exp2(byte - 127.0)
    codes = (blocks / scale).astype(np.float32).astype(dtype).astype(np.float64)
    return np.moveaxis((codes * scale).reshape(v.shape), -1, axis)


WIDE = False


def mx_kscale(k):
    if not WIDE:
        return np.ones(k)
    levels = np.array([10, -10, 5, -5, 0])
    a = np.random.permutation(np.resize(levels, k // 512 * 4)).reshape(k // 512, 4)
    idx = np.arange(k)
    return np.exp2(a[idx // 512, idx % 128 // 32])


BF16 = ml_dtypes.bfloat16


def bf(x):
    return np.asarray(x, np.float32).astype(BF16)


def f64(x):
    return np.asarray(x).astype(np.float64)


B, DETER, STOCH, ACT, HID, BLOCKS, NIN, NG = 256, 4096, 1024, 512, 512, 8, 3, 3
DPB = DETER // BLOCKS
EPS = 1e-4


def silu(v):
    return v / (1.0 + np.exp(-v))


def sigmoid(v):
    return 1.0 / (1.0 + np.exp(-v))


def rmsnorm(v, g):
    return v * (1.0 / np.sqrt(np.mean(v * v, axis=-1, keepdims=True) + EPS)) * g


def setup_inputs():
    s = mx_kscale(DETER)
    n = np.random.standard_normal
    return {"hid0": bf(silu(n((B, DETER))) * s), "deter": bf(n((B, DETER))),
            "hw1": bf(n((BLOCKS, DPB, DPB)) * 1.5 / np.sqrt(DPB) / s.reshape(BLOCKS, DPB, 1)), "hb1": bf(n(DETER) * 0.1), "hg1": bf(1.0 + n(DETER) * 0.1),
            "gw": bf(n((BLOCKS, DPB, NG * DPB)) * 2.0 / np.sqrt(DPB)), "gb": bf(n(NG * DETER) * 0.2)}


def block_linear(vq, wq, b):
    y = vq.transpose(1, 0, 2) @ wq
    return y.transpose(1, 0, 2).reshape(B, -1) + b


def reference(hid0, deter, hw1, hb1, hg1, gw, gb):
    u = block_linear(mxq(f64(hid0).reshape(B, BLOCKS, DPB), 2, "e4m3"), mxq(f64(hw1), 1, "e4m3"), f64(hb1))
    h = silu(rmsnorm(u, f64(hg1)))
    p = block_linear(mxq(h.reshape(B, BLOCKS, DPB), 2, "e4m3"), mxq(f64(gw), 1, "e4m3"), f64(gb))
    g = p.reshape(B, BLOCKS, NG, DPB)
    reset = sigmoid(g[:, :, 0, :].reshape(B, DETER))
    cand = np.tanh(reset * g[:, :, 1, :].reshape(B, DETER))
    update = sigmoid(g[:, :, 2, :].reshape(B, DETER) - 1.0)
    return update * cand + (1.0 - update) * f64(deter)

@@ -1,0 +1,438 @@
+from contextlib import ExitStack
+
+import concourse.mybir as mybir
+from concourse.masks import make_identity
+
+F32 = mybir.dt.float32
+BF16 = mybir.dt.bfloat16
+U32 = mybir.dt.uint32
+U8 = mybir.dt.uint8
+FP8X4 = mybir.dt.float8_e4m3fn_x4
+ACT = mybir.ActivationFunctionType
+ALU = mybir.AluOpType
+
+P = 128
+PACK = 4
+BATCH = 256
+BATCH_TILES = BATCH // P
+DETER = 4096
+BLOCKS = 8
+DPB = DETER // BLOCKS
+FEAT_TILES = DPB // P
+HALVES = 2
+GATES = 3
+RESET, CAND, UPDATE = 0, 1, 2
+EPS = 1e-4
+CHUNKS = BLOCKS * GATES
+UNITS = BLOCKS * HALVES
+PIECE = DPB // 2
+EARLY_CHUNKS = 2 * (BLOCKS - 1)
+GW_AHEAD = 3
+
+FLOPS = 2 * BATCH * DPB * (DPB + GATES * DPB) * BLOCKS
+
+
+def regroup(copy, grouped, rows):
+    copy(
+        out=grouped.rearrange("p (c i) t -> p c t i", i=4),
+        in_=rows.rearrange("p t (c i) -> p c t i", i=4),
+    )
+
+
+def tile_deter_pb_kernel(tc, hid0, deter, hw1, hb1, hg1, gw, gb, out):
+    nc = tc.nc
+    with ExitStack() as stack:
+        const = stack.enter_context(tc.tile_pool(name="const", bufs=1))
+        acts = stack.enter_context(tc.tile_pool(name="acts", bufs=1))
+        wraw = stack.enter_context(tc.tile_pool(name="wraw", bufs=2))
+        keep = stack.enter_context(tc.tile_pool(name="keep", bufs=1))
+        stage = stack.enter_context(tc.tile_pool(name="stage", bufs=2))
+        psum = stack.enter_context(tc.psum_pool(name="psum", bufs=1))
+        stack.enter_context(tc.manual_schedule())
+
+        n_hidden = DETER // P
+        n_gate = GATES * DETER // P
+        batch_major = "(bt p) f -> p bt f"
+
+        ident_f32 = const.tile([P, P], F32)
+        make_identity(nc, ident_f32[:])
+        ident_bf16 = const.tile([P, P], BF16)
+        make_identity(nc, ident_bf16[:])
+        ones_mean = const.tile([P, P], F32)
+        nc.vector.memset(ones_mean[:], 1.0 / DETER)
+        eps = const.tile([P, 1], F32)
+        nc.vector.memset(eps[:], EPS)
+        hidden_rows = const.tile([P, P], BF16)
+        nc.vector.memset(hidden_rows[:], 0.0)
+        gate_rows = const.tile([P, P], BF16)
+        nc.vector.memset(gate_rows[:], 0.0)
+
+        hid_codes = keep.tile([P, BLOCKS, BATCH], U32, align_bytes=64)
+        hid_scales = keep.tile([P, BLOCKS, BATCH], U8, align_bytes=64)
+        w1_codes = keep.tile([P, BLOCKS, DPB], U32, align_bytes=64)
+        w1_scales = keep.tile([P, BLOCKS, DPB], U8, align_bytes=64)
+        gw_codes = keep.tile([P, BLOCKS, GATES * DPB], U32, align_bytes=64)
+        gw_scales = keep.tile([P, BLOCKS, GATES * DPB], U8, align_bytes=64)
+
+        w1_rows = {}
+        gw_rows = {}
+
+        def load_w1_pair(pair):
+            w1_rows[pair] = wraw.tile([P, 2, PACK, DPB], BF16, name="w1_rows", tag="w1_rows")
+            nc.sync.dma_start(
+                out=w1_rows[pair][:].rearrange("p j (u e) n -> p j u (e n)", e=2),
+                in_=hw1[2 * pair : 2 * pair + 2].rearrange("j (u p e) n -> p j u (e n)", u=2, e=2),
+            )
+
+        def load_gw(block):
+            gw_rows[block] = wraw.tile(
+                [P, PACK, GATES * DPB], BF16, name="gw_rows", tag="gw_rows", bufs=GW_AHEAD
+            )
+            nc.sync.dma_start(out=gw_rows[block][:], in_=gw[block].rearrange("(t p) n -> p t n", p=P))
+
+        nc.sync.dma_start(out=hidden_rows[0:n_hidden, :], in_=hb1.rearrange("(m p) -> m p", p=P))
+        nc.sync.dma_start(
+            out=hidden_rows[n_hidden : 2 * n_hidden, :], in_=hg1.rearrange("(m p) -> m p", p=P)
+        )
+        nc.sync.dma_start(out=gate_rows[0:n_gate, :], in_=gb.rearrange("(m p) -> m p", p=P))
+        hid_sb = acts.tile([P, BATCH_TILES, DETER], BF16, tag="acts")
+        half_cols = DETER // 2
+        nc.sync.dma_start(
+            out=hid_sb[:, :, 0:half_cols], in_=hid0.rearrange(batch_major, p=P)[:, :, 0:half_cols]
+        )
+        load_w1_pair(0)
+        nc.sync.dma_start(
+            out=hid_sb[:, :, half_cols:DETER],
+            in_=hid0.rearrange(batch_major, p=P)[:, :, half_cols:DETER],
+        )
+        load_w1_pair(1)
+        load_gw(0)
+
+        hidden_cols_ps = psum.tile([P, P], BF16, tag="inT", bufs=2)
+        nc.tensor.transpose(hidden_cols_ps[:], hidden_rows[:], ident_bf16[:])
+        hidden_cols = const.tile([P, 2 * n_hidden], F32)
+        nc.vector.tensor_copy(out=hidden_cols[:], in_=hidden_cols_ps[:, 0 : 2 * n_hidden])
+        hb_cols = hidden_cols[:, 0:n_hidden]
+        hg_cols = hidden_cols[:, n_hidden : 2 * n_hidden]
+        gate_cols_ps = psum.tile([P, P], BF16, tag="inT", bufs=2)
+        nc.tensor.transpose(gate_cols_ps[:], gate_rows[:], ident_bf16[:])
+        gb_cols = const.tile([P, BLOCKS, GATES, FEAT_TILES], F32)
+        nc.vector.tensor_copy(
+            out=gb_cols[:].rearrange("p j g t -> p (j g t)"), in_=gate_cols_ps[:, 0:n_gate]
+        )
+        nc.vector.tensor_scalar_add(
+            out=gb_cols[:, :, UPDATE, :], in0=gb_cols[:, :, UPDATE, :], scalar1=-1.0
+        )
+
+        hid_words = hid_sb[:].bitcast(F32)
+        words_per_block = DPB // 2
+
+        hidT = {}
+
+        def transpose_hid0(j):
+            hidT_ps = psum.tile([P, 2, BATCH], F32, tag="inT", bufs=2)
+            hidT[j] = hidT_ps
+            for u in range(2):
+                first = j * words_per_block + u * P
+                for bt in range(BATCH_TILES):
+                    nc.tensor.transpose(
+                        hidT_ps[:, u, bt * P : (bt + 1) * P],
+                        hid_words[:, bt, first : first + P],
+                        ident_f32[:],
+                    )
+
+        def quantise_hid0(j):
+            hid_grouped = stage.tile([P, BATCH * PACK], BF16, tag="act_grouped", align_bytes=64)
+            nc.scalar.copy(
+                out=hid_grouped[:].bitcast(F32).rearrange("p (b u) -> p b u", u=2),
+                in_=hidT[j][:].rearrange("p u b -> p b u"),
+            )
+            nc.vector.quantize_mx(
+                out=hid_codes[:, j, :].bitcast(FP8X4),
+                scales=hid_scales[:, j, :],
+                in_=hid_grouped[:],
+            )
+
+        w1_grouped = {}
+
+        def regroup_w1(j):
+            w1_grouped[j] = stage.tile(
+                [P, DPB, PACK], BF16, name="w1_grouped", tag="grouped", bufs=4, align_bytes=64
+            )
+            regroup(nc.vector.tensor_copy, w1_grouped[j][:], w1_rows[j // 2][:, j % 2, :, :])
+
+        def quantise_w1(j):
+            nc.vector.quantize_mx(
+                out=w1_codes[:, j, :].bitcast(FP8X4),
+                scales=w1_scales[:, j, :],
+                in_=w1_grouped[j][:].rearrange("p w t -> p (w t)"),
+            )
+
+        gw_grouped = {}
+
+        def regroup_gw(copy, chunk, lo, hi):
+            block, gate = divmod(chunk, GATES)
+            if lo == 0:
+                gw_grouped[chunk] = stage.tile(
+                    [P, DPB, PACK], BF16, name="gw_grouped", tag="grouped", bufs=4, align_bytes=64
+                )
+            regroup(
+                copy,
+                gw_grouped[chunk][:, lo:hi, :],
+                gw_rows[block][:, :, gate * DPB + lo : gate * DPB + hi],
+            )
+            if gate == GATES - 1 and hi == DPB and block + GW_AHEAD < BLOCKS:
+                load_gw(block + GW_AHEAD)
+
+        def quantise_gw(chunk):
+            block, gate = divmod(chunk, GATES)
+            cols = slice(gate * DPB, (gate + 1) * DPB)
+            nc.vector.quantize_mx(
+                out=gw_codes[:, block, cols].bitcast(FP8X4),
+                scales=gw_scales[:, block, cols],
+                in_=gw_grouped[chunk][:].rearrange("p w t -> p (w t)"),
+            )
+
+        def late_piece(q):
+            chunk = EARLY_CHUNKS + q // 2
+            if chunk < CHUNKS:
+                regroup_gw(nc.scalar.copy, chunk, (q % 2) * PIECE, (q % 2 + 1) * PIECE)
+
+        def late_quantise(q):
+            chunk = EARLY_CHUNKS + q // 2 - 1
+            if q % 2 == 0 and EARLY_CHUNKS <= chunk < CHUNKS:
+                quantise_gw(chunk)
+
+        def hidden_matmuls(unit):
+            j, half = divmod(unit, HALVES)
+            u_ps = psum.tile([P, 2, BATCH], F32, tag="mm", bufs=5)
+            for s in range(2):
+                cols = slice((2 * half + s) * P, (2 * half + s + 1) * P)
+                nc.tensor.matmul_mx(
+                    out=u_ps[:, s, :],
+                    lhsT=w1_codes[:, j, cols].bitcast(FP8X4),
+                    lhsT_scale=w1_scales[:, j, cols],
+                    rhs=hid_codes[:, j, :].bitcast(FP8X4),
+                    rhs_scale=hid_scales[:, j, :],
+                    start=True,
+                    stop=True,
+                )
+            return u_ps
+
+        for j in range(4):
+            transpose_hid0(j)
+            quantise_hid0(j)
+        regroup_w1(0)
+        regroup_w1(1)
+        quantise_w1(0)
+        quantise_w1(1)
+        load_w1_pair(2)
+        load_gw(1)
+
+        mean_ps = psum.tile([P, BATCH], F32, tag="outT")
+        u_tiles = {}
+        for half in range(HALVES):
+            u_tiles[half] = hidden_matmuls(half)
+        for j in range(BLOCKS):
+            vector_chunk = 2 * (j - 1)
+            scalar_chunk = vector_chunk + 1
+            if j >= 2:
+                quantise_gw(scalar_chunk - 2)
+            if j + 2 < BLOCKS:
+                regroup_w1(j + 2)
+            if j == 1:
+                load_w1_pair(3)
+                load_gw(2)
+            if j + 1 < BLOCKS:
+                for half in range(HALVES):
+                    u_tiles[(j + 1) * HALVES + half] = hidden_matmuls((j + 1) * HALVES + half)
+            if j + 4 < BLOCKS:
+                transpose_hid0(j + 4)
+            if j == 3:
+                deter_sb = acts.tile([P, BATCH_TILES, DETER], BF16, tag="acts")
+                nc.sync.dma_start(out=deter_sb[:], in_=deter.rearrange(batch_major, p=P))
+            for t in range(FEAT_TILES):
+                m = j * FEAT_TILES + t
+                squares = stage.tile([P, BATCH], F32, tag="f32_tile", bufs=8)
+                nc.scalar.activation(
+                    out=squares[:],
+                    in_=u_tiles[m // 2][:, m % 2, :],
+                    func=ACT.Square,
+                    bias=hb_cols[:, m : m + 1],
+                )
+                nc.tensor.matmul(
+                    out=mean_ps[:],
+                    lhsT=ones_mean[:],
+                    rhs=squares[:],
+                    start=(m == 0),
+                    stop=(m == n_hidden - 1),
+                )
+            if j >= 1:
+                regroup_gw(nc.vector.tensor_copy, vector_chunk, 0, DPB)
+                regroup_gw(nc.scalar.copy, scalar_chunk, 0, PIECE)
+            if j + 2 < BLOCKS:
+                quantise_w1(j + 2)
+            if j + 4 < BLOCKS:
+                quantise_hid0(j + 4)
+            if j >= 1:
+                regroup_gw(nc.scalar.copy, scalar_chunk, PIECE, DPB)
+                quantise_gw(vector_chunk)
+        quantise_gw(EARLY_CHUNKS - 1)
+
+        rms = const.tile([P, BATCH], F32)
+        nc.scalar.activation(out=rms[:], in_=mean_ps[:], func=ACT.Sqrt, bias=eps[:, 0:1])
+        rstd = const.tile([P, BATCH], F32)
+        nc.vector.reciprocal(out=rstd[:], in_=rms[:])
+
+        h_codes = keep.tile([P, BLOCKS, BATCH], U32, align_bytes=64)
+        h_scales = keep.tile([P, BLOCKS, BATCH], U8, align_bytes=64)
+        h_grouped = {}
+
+        def quantise_h(j):
+            nc.vector.quantize_mx(
+                out=h_codes[:, j, :].bitcast(FP8X4),
+                scales=h_scales[:, j, :],
+                in_=h_grouped[j][:].rearrange("p w t -> p (w t)"),
+            )
+
+        for half in range(HALVES):
+            u_tiles[half] = hidden_matmuls(half)
+        for j in range(BLOCKS):
+            if j + 1 < BLOCKS:
+                for half in range(HALVES):
+                    u_tiles[(j + 1) * HALVES + half] = hidden_matmuls((j + 1) * HALVES + half)
+            h_rows = stage.tile([P, PACK, BATCH], BF16)
+            for t in range(FEAT_TILES):
+                m = j * FEAT_TILES + t
+                normed = stage.tile([P, BATCH], F32, tag="f32_tile", bufs=8)
+                nc.vector.scalar_tensor_tensor(
+                    out=normed[:],
+                    in0=u_tiles[m // 2][:, m % 2, :],
+                    scalar=hb_cols[:, m : m + 1],
+                    in1=rstd[:],
+                    op0=ALU.add,
+                    op1=ALU.mult,
+                )
+                nc.scalar.activation(
+                    out=h_rows[:, t, :], in_=normed[:], func=ACT.Silu, scale=hg_cols[:, m : m + 1]
+                )
+            if j >= 1:
+                quantise_h(j - 1)
+            late_piece(j)
+            late_quantise(j)
+            h_grouped[j] = stage.tile(
+                [P, BATCH, PACK], BF16, name="h_grouped", tag="act_grouped", align_bytes=64
+            )
+            regroup(nc.vector.tensor_copy, h_grouped[j][:], h_rows[:])
+        quantise_h(BLOCKS - 1)
+
+        out_view = out.rearrange(batch_major, p=P)
+        gate_ps = {}
+        deterT = {}
+        reset = {}
+        update = {}
+        mix = {}
+        mixT = {}
+        new_state = {}
+
+        def gate_matmuls(unit):
+            j, half = divmod(unit, HALVES)
+            for gate in (RESET, UPDATE, CAND):
+                acc = psum.tile([P, 2, BATCH], F32, tag="mm", bufs=5)
+                gate_ps[unit, gate] = acc
+                for s in range(2):
+                    first = gate * DPB + (2 * half + s) * P
+                    nc.tensor.matmul_mx(
+                        out=acc[:, s, :],
+                        lhsT=gw_codes[:, j, first : first + P].bitcast(FP8X4),
+                        lhsT_scale=gw_scales[:, j, first : first + P],
+                        rhs=h_codes[:, j, :].bitcast(FP8X4),
+                        rhs_scale=h_scales[:, j, :],
+                        start=True,
+                        stop=True,
+                    )
+
+        def transpose_deter(unit):
+            deterT[unit] = psum.tile([P, 2, BATCH], BF16, name="deterT_ps", tag="inT", bufs=2)
+            for s in range(2):
+                first = (unit * 2 + s) * P
+                for bt in range(BATCH_TILES):
+                    nc.tensor.transpose(
+                        deterT[unit][:, s, bt * P : (bt + 1) * P],
+                        deter_sb[:, bt, first : first + P],
+                        ident_bf16[:],
+                    )
+
+        def sigmoids(unit):
+            j, half = divmod(unit, HALVES)
+            reset[unit] = stage.tile([P, 2, BATCH], F32, name="reset")
+            update[unit] = stage.tile([P, 2, BATCH], F32, name="update", bufs=3)
+            for gate, result in ((RESET, reset[unit]), (UPDATE, update[unit])):
+                for s in range(2):
+                    t = 2 * half + s
+                    nc.scalar.activation(
+                        out=result[:, s, :],
+                        in_=gate_ps[unit, gate][:, s, :],
+                        func=ACT.Sigmoid,
+                        bias=gb_cols[:, j, gate, t : t + 1],
+                    )
+
+        def reset_candidate(unit):
+            j, half = divmod(unit, HALVES)
+            mix[unit] = stage.tile([P, 2, BATCH], F32, name="mix", bufs=3)
+            for s in range(2):
+                t = 2 * half + s
+                nc.vector.scalar_tensor_tensor(
+                    out=mix[unit][:, s, :],
+                    in0=gate_ps[unit, CAND][:, s, :],
+                    scalar=gb_cols[:, j, CAND, t : t + 1],
+                    in1=reset[unit][:, s, :],
+                    op0=ALU.add,
+                    op1=ALU.mult,
+                )
+
+        def mix_state(unit):
+            m = mix[unit]
+            nc.vector.tensor_tensor(out=m[:], in0=m[:], in1=deterT[unit][:], op=ALU.subtract)
+            nc.vector.tensor_tensor(out=m[:], in0=m[:], in1=update[unit][:], op=ALU.mult)
+            mixT[unit] = psum.tile([P, BATCH_TILES, 2 * P], F32, name="mixT_ps", tag="outT")
+            for s in range(2):
+                for bt in range(BATCH_TILES):
+                    nc.tensor.transpose(
+                        mixT[unit][:, bt, s * P : (s + 1) * P],
+                        m[:, s, bt * P : (bt + 1) * P],
+                        ident_f32[:],
+                    )
+
+        def finish(unit):
+            j, half = divmod(unit, HALVES)
+            if half == 0:
+                new_state[j] = stage.tile([P, BATCH_TILES, DPB], F32, name="new_state")
+            nc.vector.tensor_tensor(
+                out=new_state[j][:, :, half * 2 * P : (half + 1) * 2 * P],
+                in0=mixT[unit][:],
+                in1=deter_sb[:, :, unit * 2 * P : (unit + 1) * 2 * P],
+                op=ALU.add,
+            )
+            if half == HALVES - 1:
+                nc.sync.dma_start(out=out_view[:, :, j * DPB : (j + 1) * DPB], in_=new_state[j][:])
+
+        gate_matmuls(0)
+        transpose_deter(0)
+        for step in range(UNITS + 2):
+            if step < UNITS:
+                sigmoids(step)
+            if step + 1 < UNITS:
+                gate_matmuls(step + 1)
+            if 1 <= step <= UNITS:
+                nc.scalar.activation(out=mix[step - 1][:], in_=mix[step - 1][:], func=ACT.Tanh)
+            late_piece(BLOCKS + step)
+            if step < UNITS:
+                reset_candidate(step)
+            if step >= 2:
+                finish(step - 2)
+            if 1 <= step <= UNITS:
+                mix_state(step - 1)
+            if step + 1 < UNITS:
+                transpose_deter(step + 1)
+            late_quantise(BLOCKS + step)

@@ -79,10 +79,11 @@ def tile_deter_pb_kernel(tc, hid0, deter, hw1, hb1, hg1, gw, gb, out):
 
         def load_w1_pair(pair):
             w1_rows[pair] = wraw.tile([P, 2, PACK, DPB], BF16, name="w1_rows", tag="w1_rows")
-            nc.sync.dma_start(
-                out=w1_rows[pair][:].rearrange("p j (u e) n -> p j u (e n)", e=2),
-                in_=hw1[2 * pair : 2 * pair + 2].rearrange("j (u p e) n -> p j u (e n)", u=2, e=2),
-            )
+            for i in range(2):
+                nc.sync.dma_start(
+                    out=w1_rows[pair][:, i, :, :].rearrange("p (u e) n -> p u (e n)", e=2),
+                    in_=hw1[2 * pair + i].rearrange("(u p e) n -> p u (e n)", u=2, e=2),
+                )
 
         def load_gw(block):
             gw_rows[block] = wraw.tile(
@@ -90,39 +91,23 @@ def tile_deter_pb_kernel(tc, hid0, deter, hw1, hb1, hg1, gw, gb, out):
             )
             nc.sync.dma_start(out=gw_rows[block][:], in_=gw[block].rearrange("(t p) n -> p t n", p=P))
 
+        hid_sb = acts.tile([P, BATCH_TILES, DETER], BF16, tag="acts")
+
+        def load_hid0(first_block, n_blocks):
+            cols = slice(first_block * DPB, (first_block + n_blocks) * DPB)
+            nc.sync.dma_start(out=hid_sb[:, :, cols], in_=hid0.rearrange(batch_major, p=P)[:, :, cols])
+
+        load_hid0(0, 2)
+        load_w1_pair(0)
         nc.sync.dma_start(out=hidden_rows[0:n_hidden, :], in_=hb1.rearrange("(m p) -> m p", p=P))
         nc.sync.dma_start(
             out=hidden_rows[n_hidden : 2 * n_hidden, :], in_=hg1.rearrange("(m p) -> m p", p=P)
         )
         nc.sync.dma_start(out=gate_rows[0:n_gate, :], in_=gb.rearrange("(m p) -> m p", p=P))
-        hid_sb = acts.tile([P, BATCH_TILES, DETER], BF16, tag="acts")
-        half_cols = DETER // 2
-        nc.sync.dma_start(
-            out=hid_sb[:, :, 0:half_cols], in_=hid0.rearrange(batch_major, p=P)[:, :, 0:half_cols]
-        )
-        load_w1_pair(0)
-        nc.sync.dma_start(
-            out=hid_sb[:, :, half_cols:DETER],
-            in_=hid0.rearrange(batch_major, p=P)[:, :, half_cols:DETER],
-        )
+        load_hid0(2, 2)
         load_w1_pair(1)
+        load_hid0(4, 4)
         load_gw(0)
-
-        hidden_cols_ps = psum.tile([P, P], BF16, tag="inT", bufs=2)
-        nc.tensor.transpose(hidden_cols_ps[:], hidden_rows[:], ident_bf16[:])
-        hidden_cols = const.tile([P, 2 * n_hidden], F32)
-        nc.vector.tensor_copy(out=hidden_cols[:], in_=hidden_cols_ps[:, 0 : 2 * n_hidden])
-        hb_cols = hidden_cols[:, 0:n_hidden]
-        hg_cols = hidden_cols[:, n_hidden : 2 * n_hidden]
-        gate_cols_ps = psum.tile([P, P], BF16, tag="inT", bufs=2)
-        nc.tensor.transpose(gate_cols_ps[:], gate_rows[:], ident_bf16[:])
-        gb_cols = const.tile([P, BLOCKS, GATES, FEAT_TILES], F32)
-        nc.vector.tensor_copy(
-            out=gb_cols[:].rearrange("p j g t -> p (j g t)"), in_=gate_cols_ps[:, 0:n_gate]
-        )
-        nc.vector.tensor_scalar_add(
-            out=gb_cols[:, :, UPDATE, :], in0=gb_cols[:, :, UPDATE, :], scalar1=-1.0
-        )
 
         hid_words = hid_sb[:].bitcast(F32)
         words_per_block = DPB // 2
@@ -142,7 +127,7 @@ def tile_deter_pb_kernel(tc, hid0, deter, hw1, hb1, hg1, gw, gb, out):
                     )
 
         def quantise_hid0(j):
-            hid_grouped = stage.tile([P, BATCH * PACK], BF16, tag="act_grouped", align_bytes=64)
+            hid_grouped = stage.tile([P, BATCH * PACK], BF16, align_bytes=64)
             nc.scalar.copy(
                 out=hid_grouped[:].bitcast(F32).rearrange("p (b u) -> p b u", u=2),
                 in_=hidT[j][:].rearrange("p u b -> p b u"),
@@ -195,13 +180,19 @@ def tile_deter_pb_kernel(tc, hid0, deter, hw1, hb1, hg1, gw, gb, out):
 
         def late_piece(q):
             chunk = EARLY_CHUNKS + q // 2
+            copy = nc.scalar.copy if q % 2 == 0 else nc.vector.tensor_copy
             if chunk < CHUNKS:
-                regroup_gw(nc.scalar.copy, chunk, (q % 2) * PIECE, (q % 2 + 1) * PIECE)
+                regroup_gw(copy, chunk, (q % 2) * PIECE, (q % 2 + 1) * PIECE)
 
         def late_quantise(q):
             chunk = EARLY_CHUNKS + q // 2 - 1
             if q % 2 == 0 and EARLY_CHUNKS <= chunk < CHUNKS:
                 quantise_gw(chunk)
+
+        def gpsimd_copy(out, in_):
+            nc.gpsimd.tensor_scalar(
+                out=out, in0=in_, scalar1=1.0, scalar2=0.0, op0=ALU.mult, op1=ALU.add
+            )
 
         def hidden_matmuls(unit):
             j, half = divmod(unit, HALVES)
@@ -219,7 +210,7 @@ def tile_deter_pb_kernel(tc, hid0, deter, hw1, hb1, hg1, gw, gb, out):
                 )
             return u_ps
 
-        for j in range(4):
+        for j in range(2):
             transpose_hid0(j)
             quantise_hid0(j)
         regroup_w1(0)
@@ -228,6 +219,26 @@ def tile_deter_pb_kernel(tc, hid0, deter, hw1, hb1, hg1, gw, gb, out):
         quantise_w1(1)
         load_w1_pair(2)
         load_gw(1)
+
+        hidden_cols_ps = psum.tile([P, P], BF16, tag="inT", bufs=2)
+        nc.tensor.transpose(hidden_cols_ps[:], hidden_rows[:], ident_bf16[:])
+        hidden_cols = const.tile([P, 2 * n_hidden], F32)
+        nc.vector.tensor_copy(out=hidden_cols[:], in_=hidden_cols_ps[:, 0 : 2 * n_hidden])
+        hb_cols = hidden_cols[:, 0:n_hidden]
+        hg_cols = hidden_cols[:, n_hidden : 2 * n_hidden]
+        gate_cols_ps = psum.tile([P, P], BF16, tag="inT", bufs=2)
+        nc.tensor.transpose(gate_cols_ps[:], gate_rows[:], ident_bf16[:])
+        gb_cols = const.tile([P, BLOCKS, GATES, FEAT_TILES], F32)
+        nc.vector.tensor_copy(
+            out=gb_cols[:].rearrange("p j g t -> p (j g t)"), in_=gate_cols_ps[:, 0:n_gate]
+        )
+        nc.vector.tensor_scalar_add(
+            out=gb_cols[:, :, UPDATE, :], in0=gb_cols[:, :, UPDATE, :], scalar1=-1.0
+        )
+
+        for j in range(2, 4):
+            transpose_hid0(j)
+            quantise_hid0(j)
 
         mean_ps = psum.tile([P, BATCH], F32, tag="outT")
         u_tiles = {}
@@ -316,14 +327,14 @@ def tile_deter_pb_kernel(tc, hid0, deter, hw1, hb1, hg1, gw, gb, out):
                 nc.scalar.activation(
                     out=h_rows[:, t, :], in_=normed[:], func=ACT.Silu, scale=hg_cols[:, m : m + 1]
                 )
-            if j >= 1:
-                quantise_h(j - 1)
             late_piece(j)
             late_quantise(j)
+            if j >= 1:
+                quantise_h(j - 1)
             h_grouped[j] = stage.tile(
-                [P, BATCH, PACK], BF16, name="h_grouped", tag="act_grouped", align_bytes=64
+                [P, BATCH, PACK], BF16, name="h_grouped", bufs=1, align_bytes=64
             )
-            regroup(nc.vector.tensor_copy, h_grouped[j][:], h_rows[:])
+            regroup(gpsimd_copy, h_grouped[j][:], h_rows[:])
         quantise_h(BLOCKS - 1)
 
         out_view = out.rearrange(batch_major, p=P)
@@ -392,15 +403,20 @@ def tile_deter_pb_kernel(tc, hid0, deter, hw1, hb1, hg1, gw, gb, out):
                 )
 
         def mix_state(unit):
-            m = mix[unit]
-            nc.vector.tensor_tensor(out=m[:], in0=m[:], in1=deterT[unit][:], op=ALU.subtract)
-            nc.vector.tensor_tensor(out=m[:], in0=m[:], in1=update[unit][:], op=ALU.mult)
+            nc.vector.tensor_tensor(
+                out=mix[unit][:], in0=mix[unit][:], in1=deterT[unit][:], op=ALU.subtract
+            )
+            nc.gpsimd.tensor_tensor(
+                out=mix[unit][:], in0=mix[unit][:], in1=update[unit][:], op=ALU.mult
+            )
+
+        def transpose_mix(unit):
             mixT[unit] = psum.tile([P, BATCH_TILES, 2 * P], F32, name="mixT_ps", tag="outT")
             for s in range(2):
                 for bt in range(BATCH_TILES):
                     nc.tensor.transpose(
                         mixT[unit][:, bt, s * P : (s + 1) * P],
-                        m[:, s, bt * P : (bt + 1) * P],
+                        mix[unit][:, s, bt * P : (bt + 1) * P],
                         ident_f32[:],
                     )
 
@@ -419,20 +435,22 @@ def tile_deter_pb_kernel(tc, hid0, deter, hw1, hb1, hg1, gw, gb, out):
 
         gate_matmuls(0)
         transpose_deter(0)
-        for step in range(UNITS + 2):
+        for step in range(UNITS + 3):
             if step < UNITS:
                 sigmoids(step)
             if step + 1 < UNITS:
                 gate_matmuls(step + 1)
             if 1 <= step <= UNITS:
                 nc.scalar.activation(out=mix[step - 1][:], in_=mix[step - 1][:], func=ACT.Tanh)
-            late_piece(BLOCKS + step)
             if step < UNITS:
                 reset_candidate(step)
-            if step >= 2:
-                finish(step - 2)
+            if step >= 3:
+                finish(step - 3)
+            if 2 <= step <= UNITS + 1:
+                transpose_mix(step - 2)
+            late_piece(BLOCKS + step)
+            late_quantise(BLOCKS + step)
             if 1 <= step <= UNITS:
                 mix_state(step - 1)
             if step + 1 < UNITS:
                 transpose_deter(step + 1)
-            late_quantise(BLOCKS + step)

@@ -26,8 +26,10 @@ EPS = 1e-4
 CHUNKS = BLOCKS * GATES
 UNITS = BLOCKS * HALVES
 PIECE = DPB // 2
-EARLY_CHUNKS = 2 * (BLOCKS - 1)
+EARLY_CHUNKS = 2 * (BLOCKS - 2)
+VECTOR_WAIT_PIECES = 4
 GW_AHEAD = 3
+PSUM_BUFS = {"mm": 5, "inT": 2, "outT": 1}
 
 FLOPS = 2 * BATCH * DPB * (DPB + GATES * DPB) * BLOCKS
 
@@ -91,22 +93,25 @@ def tile_deter_pb_kernel(tc, hid0, deter, hw1, hb1, hg1, gw, gb, out):
             )
             nc.sync.dma_start(out=gw_rows[block][:], in_=gw[block].rearrange("(t p) n -> p t n", p=P))
 
-        hid_sb = acts.tile([P, BATCH_TILES, DETER], BF16, tag="acts")
+        hid_sb = acts.tile([P, BLOCKS // 2, BATCH_TILES, 2 * DPB], BF16, tag="acts")
 
-        def load_hid0(first_block, n_blocks):
-            cols = slice(first_block * DPB, (first_block + n_blocks) * DPB)
-            nc.sync.dma_start(out=hid_sb[:, :, cols], in_=hid0.rearrange(batch_major, p=P)[:, :, cols])
+        def load_hid0(pair):
+            cols = slice(pair * 2 * DPB, (pair + 1) * 2 * DPB)
+            nc.sync.dma_start(
+                out=hid_sb[:, pair, :, :], in_=hid0.rearrange(batch_major, p=P)[:, :, cols]
+            )
 
-        load_hid0(0, 2)
+        load_hid0(0)
         load_w1_pair(0)
         nc.sync.dma_start(out=hidden_rows[0:n_hidden, :], in_=hb1.rearrange("(m p) -> m p", p=P))
         nc.sync.dma_start(
             out=hidden_rows[n_hidden : 2 * n_hidden, :], in_=hg1.rearrange("(m p) -> m p", p=P)
         )
         nc.sync.dma_start(out=gate_rows[0:n_gate, :], in_=gb.rearrange("(m p) -> m p", p=P))
-        load_hid0(2, 2)
+        load_hid0(1)
         load_w1_pair(1)
-        load_hid0(4, 4)
+        load_hid0(2)
+        load_hid0(3)
         load_gw(0)
 
         hid_words = hid_sb[:].bitcast(F32)
@@ -118,11 +123,11 @@ def tile_deter_pb_kernel(tc, hid0, deter, hw1, hb1, hg1, gw, gb, out):
             hidT_ps = psum.tile([P, 2, BATCH], F32, tag="inT", bufs=2)
             hidT[j] = hidT_ps
             for u in range(2):
-                first = j * words_per_block + u * P
+                first = (j % 2) * words_per_block + u * P
                 for bt in range(BATCH_TILES):
                     nc.tensor.transpose(
                         hidT_ps[:, u, bt * P : (bt + 1) * P],
-                        hid_words[:, bt, first : first + P],
+                        hid_words[:, j // 2, bt, first : first + P],
                         ident_f32[:],
                     )
 
@@ -140,11 +145,11 @@ def tile_deter_pb_kernel(tc, hid0, deter, hw1, hb1, hg1, gw, gb, out):
 
         w1_grouped = {}
 
-        def regroup_w1(j):
+        def regroup_w1(copy, j):
             w1_grouped[j] = stage.tile(
                 [P, DPB, PACK], BF16, name="w1_grouped", tag="grouped", bufs=4, align_bytes=64
             )
-            regroup(nc.vector.tensor_copy, w1_grouped[j][:], w1_rows[j // 2][:, j % 2, :, :])
+            regroup(copy, w1_grouped[j][:], w1_rows[j // 2][:, j % 2, :, :])
 
         def quantise_w1(j):
             nc.vector.quantize_mx(
@@ -178,9 +183,14 @@ def tile_deter_pb_kernel(tc, hid0, deter, hw1, hb1, hg1, gw, gb, out):
                 in_=gw_grouped[chunk][:].rearrange("p w t -> p (w t)"),
             )
 
-        def late_piece(q):
+        def gpsimd_copy(out, in_):
+            nc.gpsimd.tensor_scalar(
+                out=out, in0=in_, scalar1=1.0, scalar2=0.0, op0=ALU.mult, op1=ALU.add
+            )
+
+        def late_piece(q, odd_copy):
             chunk = EARLY_CHUNKS + q // 2
-            copy = nc.scalar.copy if q % 2 == 0 else nc.vector.tensor_copy
+            copy = nc.scalar.copy if q % 2 == 0 else odd_copy
             if chunk < CHUNKS:
                 regroup_gw(copy, chunk, (q % 2) * PIECE, (q % 2 + 1) * PIECE)
 
@@ -188,11 +198,6 @@ def tile_deter_pb_kernel(tc, hid0, deter, hw1, hb1, hg1, gw, gb, out):
             chunk = EARLY_CHUNKS + q // 2 - 1
             if q % 2 == 0 and EARLY_CHUNKS <= chunk < CHUNKS:
                 quantise_gw(chunk)
-
-        def gpsimd_copy(out, in_):
-            nc.gpsimd.tensor_scalar(
-                out=out, in0=in_, scalar1=1.0, scalar2=0.0, op0=ALU.mult, op1=ALU.add
-            )
 
         def hidden_matmuls(unit):
             j, half = divmod(unit, HALVES)
@@ -213,20 +218,16 @@ def tile_deter_pb_kernel(tc, hid0, deter, hw1, hb1, hg1, gw, gb, out):
         for j in range(2):
             transpose_hid0(j)
             quantise_hid0(j)
-        regroup_w1(0)
-        regroup_w1(1)
-        quantise_w1(0)
-        quantise_w1(1)
-        load_w1_pair(2)
-        load_gw(1)
+        regroup_w1(nc.vector.tensor_copy, 0)
+        regroup_w1(nc.scalar.copy, 1)
 
-        hidden_cols_ps = psum.tile([P, P], BF16, tag="inT", bufs=2)
+        hidden_cols_ps = psum.tile([P, P], BF16, tag="mm", bufs=5)
         nc.tensor.transpose(hidden_cols_ps[:], hidden_rows[:], ident_bf16[:])
         hidden_cols = const.tile([P, 2 * n_hidden], F32)
         nc.vector.tensor_copy(out=hidden_cols[:], in_=hidden_cols_ps[:, 0 : 2 * n_hidden])
         hb_cols = hidden_cols[:, 0:n_hidden]
         hg_cols = hidden_cols[:, n_hidden : 2 * n_hidden]
-        gate_cols_ps = psum.tile([P, P], BF16, tag="inT", bufs=2)
+        gate_cols_ps = psum.tile([P, P], BF16, tag="mm", bufs=5)
         nc.tensor.transpose(gate_cols_ps[:], gate_rows[:], ident_bf16[:])
         gb_cols = const.tile([P, BLOCKS, GATES, FEAT_TILES], F32)
         nc.vector.tensor_copy(
@@ -238,19 +239,24 @@ def tile_deter_pb_kernel(tc, hid0, deter, hw1, hb1, hg1, gw, gb, out):
 
         for j in range(2, 4):
             transpose_hid0(j)
-            quantise_hid0(j)
-
-        mean_ps = psum.tile([P, BATCH], F32, tag="outT")
+        quantise_w1(0)
         u_tiles = {}
         for half in range(HALVES):
             u_tiles[half] = hidden_matmuls(half)
+        for j in range(2, 4):
+            quantise_hid0(j)
+        quantise_w1(1)
+        load_w1_pair(2)
+        load_gw(1)
+
+        mean_ps = psum.tile([P, BATCH], F32, tag="outT")
         for j in range(BLOCKS):
             vector_chunk = 2 * (j - 1)
             scalar_chunk = vector_chunk + 1
             if j >= 2:
                 quantise_gw(scalar_chunk - 2)
             if j + 2 < BLOCKS:
-                regroup_w1(j + 2)
+                regroup_w1(nc.vector.tensor_copy, j + 2)
             if j == 1:
                 load_w1_pair(3)
                 load_gw(2)
@@ -278,22 +284,26 @@ def tile_deter_pb_kernel(tc, hid0, deter, hw1, hb1, hg1, gw, gb, out):
                     start=(m == 0),
                     stop=(m == n_hidden - 1),
                 )
-            if j >= 1:
+            if 1 <= j < BLOCKS - 1:
                 regroup_gw(nc.vector.tensor_copy, vector_chunk, 0, DPB)
                 regroup_gw(nc.scalar.copy, scalar_chunk, 0, PIECE)
             if j + 2 < BLOCKS:
                 quantise_w1(j + 2)
             if j + 4 < BLOCKS:
                 quantise_hid0(j + 4)
-            if j >= 1:
+            if 1 <= j < BLOCKS - 1:
                 regroup_gw(nc.scalar.copy, scalar_chunk, PIECE, DPB)
                 quantise_gw(vector_chunk)
-        quantise_gw(EARLY_CHUNKS - 1)
+        for q in range(VECTOR_WAIT_PIECES):
+            regroup_gw(
+                nc.vector.tensor_copy, EARLY_CHUNKS + q // 2, (q % 2) * PIECE, (q % 2 + 1) * PIECE
+            )
 
         rms = const.tile([P, BATCH], F32)
         nc.scalar.activation(out=rms[:], in_=mean_ps[:], func=ACT.Sqrt, bias=eps[:, 0:1])
         rstd = const.tile([P, BATCH], F32)
         nc.vector.reciprocal(out=rstd[:], in_=rms[:])
+        late_quantise(2)
 
         h_codes = keep.tile([P, BLOCKS, BATCH], U32, align_bytes=64)
         h_scales = keep.tile([P, BLOCKS, BATCH], U8, align_bytes=64)
@@ -327,15 +337,14 @@ def tile_deter_pb_kernel(tc, hid0, deter, hw1, hb1, hg1, gw, gb, out):
                 nc.scalar.activation(
                     out=h_rows[:, t, :], in_=normed[:], func=ACT.Silu, scale=hg_cols[:, m : m + 1]
                 )
-            late_piece(j)
-            late_quantise(j)
+            late_piece(VECTOR_WAIT_PIECES + j, nc.vector.tensor_copy)
+            late_quantise(VECTOR_WAIT_PIECES + j)
             if j >= 1:
                 quantise_h(j - 1)
             h_grouped[j] = stage.tile(
                 [P, BATCH, PACK], BF16, name="h_grouped", bufs=1, align_bytes=64
             )
             regroup(gpsimd_copy, h_grouped[j][:], h_rows[:])
-        quantise_h(BLOCKS - 1)
 
         out_view = out.rearrange(batch_major, p=P)
         gate_ps = {}
@@ -344,7 +353,6 @@ def tile_deter_pb_kernel(tc, hid0, deter, hw1, hb1, hg1, gw, gb, out):
         update = {}
         mix = {}
         mixT = {}
-        new_state = {}
 
         def gate_matmuls(unit):
             j, half = divmod(unit, HALVES)
@@ -402,16 +410,16 @@ def tile_deter_pb_kernel(tc, hid0, deter, hw1, hb1, hg1, gw, gb, out):
                     op1=ALU.mult,
                 )
 
-        def mix_state(unit):
+        def mix_state(unit, multiplier):
             nc.vector.tensor_tensor(
                 out=mix[unit][:], in0=mix[unit][:], in1=deterT[unit][:], op=ALU.subtract
             )
-            nc.gpsimd.tensor_tensor(
+            multiplier.tensor_tensor(
                 out=mix[unit][:], in0=mix[unit][:], in1=update[unit][:], op=ALU.mult
             )
 
-        def transpose_mix(unit):
-            mixT[unit] = psum.tile([P, BATCH_TILES, 2 * P], F32, name="mixT_ps", tag="outT")
+        def transpose_mix(unit, tag):
+            mixT[unit] = psum.tile([P, BATCH_TILES, 2 * P], F32, name="mixT_ps", tag=tag, bufs=PSUM_BUFS[tag])
             for s in range(2):
                 for bt in range(BATCH_TILES):
                     nc.tensor.transpose(
@@ -421,36 +429,39 @@ def tile_deter_pb_kernel(tc, hid0, deter, hw1, hb1, hg1, gw, gb, out):
                     )
 
         def finish(unit):
-            j, half = divmod(unit, HALVES)
-            if half == 0:
-                new_state[j] = stage.tile([P, BATCH_TILES, DPB], F32, name="new_state")
+            cols = slice(unit * 2 * P, (unit + 1) * 2 * P)
+            new_state = stage.tile([P, BATCH_TILES, 2 * P], F32, bufs=3)
             nc.vector.tensor_tensor(
-                out=new_state[j][:, :, half * 2 * P : (half + 1) * 2 * P],
-                in0=mixT[unit][:],
-                in1=deter_sb[:, :, unit * 2 * P : (unit + 1) * 2 * P],
-                op=ALU.add,
+                out=new_state[:], in0=mixT[unit][:], in1=deter_sb[:, :, cols], op=ALU.add
             )
-            if half == HALVES - 1:
-                nc.sync.dma_start(out=out_view[:, :, j * DPB : (j + 1) * DPB], in_=new_state[j][:])
+            nc.sync.dma_start(out=out_view[:, :, cols], in_=new_state[:])
 
         gate_matmuls(0)
         transpose_deter(0)
-        for step in range(UNITS + 3):
-            if step < UNITS:
-                sigmoids(step)
+        for step in range(UNITS):
+            sigmoids(step)
             if step + 1 < UNITS:
                 gate_matmuls(step + 1)
-            if 1 <= step <= UNITS:
+            if step >= 1:
                 nc.scalar.activation(out=mix[step - 1][:], in_=mix[step - 1][:], func=ACT.Tanh)
-            if step < UNITS:
-                reset_candidate(step)
+            reset_candidate(step)
             if step >= 3:
                 finish(step - 3)
-            if 2 <= step <= UNITS + 1:
-                transpose_mix(step - 2)
-            late_piece(BLOCKS + step)
-            late_quantise(BLOCKS + step)
-            if 1 <= step <= UNITS:
-                mix_state(step - 1)
+            if step >= 2:
+                transpose_mix(step - 2, "outT")
+            if step == 0:
+                quantise_h(BLOCKS - 1)
+            late_piece(VECTOR_WAIT_PIECES + BLOCKS + step, gpsimd_copy)
+            late_quantise(VECTOR_WAIT_PIECES + BLOCKS + step)
+            if step >= 1:
+                mix_state(step - 1, nc.gpsimd)
             if step + 1 < UNITS:
                 transpose_deter(step + 1)
+        last = UNITS - 1
+        nc.scalar.activation(out=mix[last][:], in_=mix[last][:], func=ACT.Tanh)
+        finish(last - 2)
+        transpose_mix(last - 1, "outT")
+        mix_state(last, nc.vector)
+        transpose_mix(last, "inT")
+        finish(last - 1)
+        finish(last)

@@ -13,23 +13,42 @@ ALU = mybir.AluOpType
 
 P = 128
 PACK = 4
+WORDS = PACK // 2
 BATCH = 256
 BATCH_TILES = BATCH // P
 DETER = 4096
 BLOCKS = 8
 DPB = DETER // BLOCKS
 FEAT_TILES = DPB // P
-HALVES = 2
+N_TILES = DETER // P
 GATES = 3
 RESET, CAND, UPDATE = 0, 1, 2
 EPS = 1e-4
+
+TILES_PER_UNIT = 2
+UNITS_PER_BLOCK = FEAT_TILES // TILES_PER_UNIT
+UNITS = BLOCKS * UNITS_PER_BLOCK
+UNIT_COLS = TILES_PER_UNIT * P
+
 CHUNKS = BLOCKS * GATES
-UNITS = BLOCKS * HALVES
 PIECE = DPB // 2
 EARLY_CHUNKS = 2 * (BLOCKS - 2)
-VECTOR_WAIT_PIECES = 4
+WAIT_CHUNKS = 2
+FIRST_LATE_CHUNK = EARLY_CHUNKS + WAIT_CHUNKS
+
+PAIR = 2
+PAIRS = BLOCKS // PAIR
+W1_PAIRS_AHEAD = 2
 GW_AHEAD = 3
+HID_AHEAD = 4
+W1_AHEAD = 2
+
 PSUM_BUFS = {"mm": 5, "inT": 2, "outT": 1}
+STAGE_BUFS = 2
+GROUPED_BUFS = 4
+F32_TILE_BUFS = 2 * FEAT_TILES
+STEPS_ALIVE = 3
+STORE_BUFS = 3
 
 FLOPS = 2 * BATCH * DPB * (DPB + GATES * DPB) * BLOCKS
 
@@ -46,22 +65,23 @@ def tile_deter_pb_kernel(tc, hid0, deter, hw1, hb1, hg1, gw, gb, out):
     with ExitStack() as stack:
         const = stack.enter_context(tc.tile_pool(name="const", bufs=1))
         acts = stack.enter_context(tc.tile_pool(name="acts", bufs=1))
-        wraw = stack.enter_context(tc.tile_pool(name="wraw", bufs=2))
+        wraw = stack.enter_context(tc.tile_pool(name="wraw", bufs=1))
         keep = stack.enter_context(tc.tile_pool(name="keep", bufs=1))
-        stage = stack.enter_context(tc.tile_pool(name="stage", bufs=2))
+        stage = stack.enter_context(tc.tile_pool(name="stage", bufs=STAGE_BUFS))
         psum = stack.enter_context(tc.psum_pool(name="psum", bufs=1))
         stack.enter_context(tc.manual_schedule())
 
-        n_hidden = DETER // P
-        n_gate = GATES * DETER // P
+        def psum_tile(shape, dtype, tag):
+            return psum.tile(shape, dtype, name=tag + "_ps", tag=tag, bufs=PSUM_BUFS[tag])
+
         batch_major = "(bt p) f -> p bt f"
 
         ident_f32 = const.tile([P, P], F32)
         make_identity(nc, ident_f32[:])
         ident_bf16 = const.tile([P, P], BF16)
         make_identity(nc, ident_bf16[:])
-        ones_mean = const.tile([P, P], F32)
-        nc.vector.memset(ones_mean[:], 1.0 / DETER)
+        mean_weights = const.tile([P, P], F32)
+        nc.vector.memset(mean_weights[:], 1.0 / DETER)
         eps = const.tile([P, 1], F32)
         nc.vector.memset(eps[:], EPS)
         hidden_rows = const.tile([P, P], BF16)
@@ -73,41 +93,46 @@ def tile_deter_pb_kernel(tc, hid0, deter, hw1, hb1, hg1, gw, gb, out):
         hid_scales = keep.tile([P, BLOCKS, BATCH], U8, align_bytes=64)
         w1_codes = keep.tile([P, BLOCKS, DPB], U32, align_bytes=64)
         w1_scales = keep.tile([P, BLOCKS, DPB], U8, align_bytes=64)
+        h_codes = keep.tile([P, BLOCKS, BATCH], U32, align_bytes=64)
+        h_scales = keep.tile([P, BLOCKS, BATCH], U8, align_bytes=64)
         gw_codes = keep.tile([P, BLOCKS, GATES * DPB], U32, align_bytes=64)
         gw_scales = keep.tile([P, BLOCKS, GATES * DPB], U8, align_bytes=64)
 
+        hid_sb = acts.tile([P, PAIRS, BATCH_TILES, PAIR * DPB], BF16, tag="acts")
         w1_rows = {}
         gw_rows = {}
 
-        def load_w1_pair(pair):
-            w1_rows[pair] = wraw.tile([P, 2, PACK, DPB], BF16, name="w1_rows", tag="w1_rows")
-            for i in range(2):
-                nc.sync.dma_start(
-                    out=w1_rows[pair][:, i, :, :].rearrange("p (u e) n -> p u (e n)", e=2),
-                    in_=hw1[2 * pair + i].rearrange("(u p e) n -> p u (e n)", u=2, e=2),
-                )
-
-        def load_gw(block):
-            gw_rows[block] = wraw.tile(
-                [P, PACK, GATES * DPB], BF16, name="gw_rows", tag="gw_rows", bufs=GW_AHEAD
-            )
-            nc.sync.dma_start(out=gw_rows[block][:], in_=gw[block].rearrange("(t p) n -> p t n", p=P))
-
-        hid_sb = acts.tile([P, BLOCKS // 2, BATCH_TILES, 2 * DPB], BF16, tag="acts")
-
         def load_hid0(pair):
-            cols = slice(pair * 2 * DPB, (pair + 1) * 2 * DPB)
+            cols = slice(pair * PAIR * DPB, (pair + 1) * PAIR * DPB)
             nc.sync.dma_start(
                 out=hid_sb[:, pair, :, :], in_=hid0.rearrange(batch_major, p=P)[:, :, cols]
             )
 
+        def load_w1_pair(pair):
+            w1_rows[pair] = wraw.tile(
+                [P, PAIR, PACK, DPB], BF16, name="w1_rows", bufs=W1_PAIRS_AHEAD
+            )
+            for i in range(PAIR):
+                nc.sync.dma_start(
+                    out=w1_rows[pair][:, i, :, :].rearrange("p (u e) n -> p u (e n)", e=2),
+                    in_=hw1[PAIR * pair + i].rearrange("(u p e) n -> p u (e n)", u=WORDS, e=2),
+                )
+
+        def load_gw(block):
+            gw_rows[block] = wraw.tile(
+                [P, PACK, GATES * DPB], BF16, name="gw_rows", bufs=GW_AHEAD
+            )
+            nc.sync.dma_start(out=gw_rows[block][:], in_=gw[block].rearrange("(t p) n -> p t n", p=P))
+
         load_hid0(0)
         load_w1_pair(0)
-        nc.sync.dma_start(out=hidden_rows[0:n_hidden, :], in_=hb1.rearrange("(m p) -> m p", p=P))
+        nc.sync.dma_start(out=hidden_rows[0:N_TILES, :], in_=hb1.rearrange("(m p) -> m p", p=P))
         nc.sync.dma_start(
-            out=hidden_rows[n_hidden : 2 * n_hidden, :], in_=hg1.rearrange("(m p) -> m p", p=P)
+            out=hidden_rows[N_TILES : 2 * N_TILES, :], in_=hg1.rearrange("(m p) -> m p", p=P)
         )
-        nc.sync.dma_start(out=gate_rows[0:n_gate, :], in_=gb.rearrange("(m p) -> m p", p=P))
+        nc.sync.dma_start(
+            out=gate_rows[0 : GATES * N_TILES, :], in_=gb.rearrange("(m p) -> m p", p=P)
+        )
         load_hid0(1)
         load_w1_pair(1)
         load_hid0(2)
@@ -116,25 +141,24 @@ def tile_deter_pb_kernel(tc, hid0, deter, hw1, hb1, hg1, gw, gb, out):
 
         hid_words = hid_sb[:].bitcast(F32)
         words_per_block = DPB // 2
-
         hidT = {}
 
         def transpose_hid0(j):
-            hidT_ps = psum.tile([P, 2, BATCH], F32, tag="inT", bufs=2)
-            hidT[j] = hidT_ps
-            for u in range(2):
-                first = (j % 2) * words_per_block + u * P
+            pair, i = divmod(j, PAIR)
+            hidT[j] = psum_tile([P, WORDS, BATCH], F32, "inT")
+            for u in range(WORDS):
+                first = i * words_per_block + u * P
                 for bt in range(BATCH_TILES):
                     nc.tensor.transpose(
-                        hidT_ps[:, u, bt * P : (bt + 1) * P],
-                        hid_words[:, j // 2, bt, first : first + P],
+                        hidT[j][:, u, bt * P : (bt + 1) * P],
+                        hid_words[:, pair, bt, first : first + P],
                         ident_f32[:],
                     )
 
         def quantise_hid0(j):
             hid_grouped = stage.tile([P, BATCH * PACK], BF16, align_bytes=64)
             nc.scalar.copy(
-                out=hid_grouped[:].bitcast(F32).rearrange("p (b u) -> p b u", u=2),
+                out=hid_grouped[:].bitcast(F32).rearrange("p (b u) -> p b u", u=WORDS),
                 in_=hidT[j][:].rearrange("p u b -> p b u"),
             )
             nc.vector.quantize_mx(
@@ -143,13 +167,20 @@ def tile_deter_pb_kernel(tc, hid0, deter, hw1, hb1, hg1, gw, gb, out):
                 in_=hid_grouped[:],
             )
 
+        def grouped_tile():
+            return stage.tile(
+                [P, DPB, PACK], BF16, name="grouped", bufs=GROUPED_BUFS, align_bytes=64
+            )
+
         w1_grouped = {}
 
         def regroup_w1(copy, j):
-            w1_grouped[j] = stage.tile(
-                [P, DPB, PACK], BF16, name="w1_grouped", tag="grouped", bufs=4, align_bytes=64
-            )
-            regroup(copy, w1_grouped[j][:], w1_rows[j // 2][:, j % 2, :, :])
+            pair, i = divmod(j, PAIR)
+            w1_grouped[j] = grouped_tile()
+            regroup(copy, w1_grouped[j][:], w1_rows[pair][:, i, :, :])
+            if i == PAIR - 1 and pair + W1_PAIRS_AHEAD < PAIRS:
+                load_w1_pair(pair + W1_PAIRS_AHEAD)
+                load_gw(pair + 1)
 
         def quantise_w1(j):
             nc.vector.quantize_mx(
@@ -163,9 +194,7 @@ def tile_deter_pb_kernel(tc, hid0, deter, hw1, hb1, hg1, gw, gb, out):
         def regroup_gw(copy, chunk, lo, hi):
             block, gate = divmod(chunk, GATES)
             if lo == 0:
-                gw_grouped[chunk] = stage.tile(
-                    [P, DPB, PACK], BF16, name="gw_grouped", tag="grouped", bufs=4, align_bytes=64
-                )
+                gw_grouped[chunk] = grouped_tile()
             regroup(
                 copy,
                 gw_grouped[chunk][:, lo:hi, :],
@@ -189,124 +218,112 @@ def tile_deter_pb_kernel(tc, hid0, deter, hw1, hb1, hg1, gw, gb, out):
             )
 
         def late_piece(q, odd_copy):
-            chunk = EARLY_CHUNKS + q // 2
-            copy = nc.scalar.copy if q % 2 == 0 else odd_copy
-            if chunk < CHUNKS:
-                regroup_gw(copy, chunk, (q % 2) * PIECE, (q % 2 + 1) * PIECE)
+            chunk, half = divmod(q, 2)
+            copy = nc.scalar.copy if half == 0 else odd_copy
+            if FIRST_LATE_CHUNK + chunk < CHUNKS:
+                regroup_gw(copy, FIRST_LATE_CHUNK + chunk, half * PIECE, (half + 1) * PIECE)
 
         def late_quantise(q):
-            chunk = EARLY_CHUNKS + q // 2 - 1
-            if q % 2 == 0 and EARLY_CHUNKS <= chunk < CHUNKS:
-                quantise_gw(chunk)
+            chunk, half = divmod(q, 2)
+            if half == 0 and FIRST_LATE_CHUNK + chunk - 1 < CHUNKS:
+                quantise_gw(FIRST_LATE_CHUNK + chunk - 1)
 
-        def hidden_matmuls(unit):
-            j, half = divmod(unit, HALVES)
-            u_ps = psum.tile([P, 2, BATCH], F32, tag="mm", bufs=5)
-            for s in range(2):
-                cols = slice((2 * half + s) * P, (2 * half + s + 1) * P)
-                nc.tensor.matmul_mx(
-                    out=u_ps[:, s, :],
-                    lhsT=w1_codes[:, j, cols].bitcast(FP8X4),
-                    lhsT_scale=w1_scales[:, j, cols],
-                    rhs=hid_codes[:, j, :].bitcast(FP8X4),
-                    rhs_scale=hid_scales[:, j, :],
-                    start=True,
-                    stop=True,
-                )
-            return u_ps
+        u_ps = {}
 
-        for j in range(2):
+        def hidden_matmuls(j):
+            for unit in range(j * UNITS_PER_BLOCK, (j + 1) * UNITS_PER_BLOCK):
+                u_ps[unit] = psum_tile([P, TILES_PER_UNIT, BATCH], F32, "mm")
+                for s in range(TILES_PER_UNIT):
+                    first = (unit * TILES_PER_UNIT + s) * P - j * DPB
+                    nc.tensor.matmul_mx(
+                        out=u_ps[unit][:, s, :],
+                        lhsT=w1_codes[:, j, first : first + P].bitcast(FP8X4),
+                        lhsT_scale=w1_scales[:, j, first : first + P],
+                        rhs=hid_codes[:, j, :].bitcast(FP8X4),
+                        rhs_scale=hid_scales[:, j, :],
+                        start=True,
+                        stop=True,
+                    )
+
+        def u_tile(m):
+            return u_ps[m // TILES_PER_UNIT][:, m % TILES_PER_UNIT, :]
+
+        for j in range(PAIR):
             transpose_hid0(j)
             quantise_hid0(j)
         regroup_w1(nc.vector.tensor_copy, 0)
         regroup_w1(nc.scalar.copy, 1)
 
-        hidden_cols_ps = psum.tile([P, P], BF16, tag="mm", bufs=5)
+        hidden_cols_ps = psum_tile([P, P], BF16, "mm")
         nc.tensor.transpose(hidden_cols_ps[:], hidden_rows[:], ident_bf16[:])
-        hidden_cols = const.tile([P, 2 * n_hidden], F32)
-        nc.vector.tensor_copy(out=hidden_cols[:], in_=hidden_cols_ps[:, 0 : 2 * n_hidden])
-        hb_cols = hidden_cols[:, 0:n_hidden]
-        hg_cols = hidden_cols[:, n_hidden : 2 * n_hidden]
-        gate_cols_ps = psum.tile([P, P], BF16, tag="mm", bufs=5)
+        hidden_cols = const.tile([P, 2 * N_TILES], F32)
+        nc.vector.tensor_copy(out=hidden_cols[:], in_=hidden_cols_ps[:, 0 : 2 * N_TILES])
+        hb_cols = hidden_cols[:, 0:N_TILES]
+        hg_cols = hidden_cols[:, N_TILES : 2 * N_TILES]
+        gate_cols_ps = psum_tile([P, P], BF16, "mm")
         nc.tensor.transpose(gate_cols_ps[:], gate_rows[:], ident_bf16[:])
         gb_cols = const.tile([P, BLOCKS, GATES, FEAT_TILES], F32)
         nc.vector.tensor_copy(
-            out=gb_cols[:].rearrange("p j g t -> p (j g t)"), in_=gate_cols_ps[:, 0:n_gate]
+            out=gb_cols[:].rearrange("p j g t -> p (j g t)"), in_=gate_cols_ps[:, 0 : GATES * N_TILES]
         )
         nc.vector.tensor_scalar_add(
             out=gb_cols[:, :, UPDATE, :], in0=gb_cols[:, :, UPDATE, :], scalar1=-1.0
         )
 
-        for j in range(2, 4):
+        for j in range(PAIR, HID_AHEAD):
             transpose_hid0(j)
         quantise_w1(0)
-        u_tiles = {}
-        for half in range(HALVES):
-            u_tiles[half] = hidden_matmuls(half)
-        for j in range(2, 4):
+        hidden_matmuls(0)
+        for j in range(PAIR, HID_AHEAD):
             quantise_hid0(j)
         quantise_w1(1)
-        load_w1_pair(2)
-        load_gw(1)
 
-        mean_ps = psum.tile([P, BATCH], F32, tag="outT")
+        mean_ps = psum_tile([P, BATCH], F32, "outT")
         for j in range(BLOCKS):
+            with_chunks = 1 <= j < BLOCKS - 1
             vector_chunk = 2 * (j - 1)
             scalar_chunk = vector_chunk + 1
             if j >= 2:
                 quantise_gw(scalar_chunk - 2)
-            if j + 2 < BLOCKS:
-                regroup_w1(nc.vector.tensor_copy, j + 2)
-            if j == 1:
-                load_w1_pair(3)
-                load_gw(2)
+            if j + W1_AHEAD < BLOCKS:
+                regroup_w1(nc.vector.tensor_copy, j + W1_AHEAD)
             if j + 1 < BLOCKS:
-                for half in range(HALVES):
-                    u_tiles[(j + 1) * HALVES + half] = hidden_matmuls((j + 1) * HALVES + half)
-            if j + 4 < BLOCKS:
-                transpose_hid0(j + 4)
-            if j == 3:
+                hidden_matmuls(j + 1)
+            if j + HID_AHEAD < BLOCKS:
+                transpose_hid0(j + HID_AHEAD)
+            if j + HID_AHEAD == BLOCKS - 1:
                 deter_sb = acts.tile([P, BATCH_TILES, DETER], BF16, tag="acts")
                 nc.sync.dma_start(out=deter_sb[:], in_=deter.rearrange(batch_major, p=P))
-            for t in range(FEAT_TILES):
-                m = j * FEAT_TILES + t
-                squares = stage.tile([P, BATCH], F32, tag="f32_tile", bufs=8)
+            for m in range(j * FEAT_TILES, (j + 1) * FEAT_TILES):
+                squares = stage.tile([P, BATCH], F32, tag="f32_tile", bufs=F32_TILE_BUFS)
                 nc.scalar.activation(
-                    out=squares[:],
-                    in_=u_tiles[m // 2][:, m % 2, :],
-                    func=ACT.Square,
-                    bias=hb_cols[:, m : m + 1],
+                    out=squares[:], in_=u_tile(m), func=ACT.Square, bias=hb_cols[:, m : m + 1]
                 )
                 nc.tensor.matmul(
                     out=mean_ps[:],
-                    lhsT=ones_mean[:],
+                    lhsT=mean_weights[:],
                     rhs=squares[:],
                     start=(m == 0),
-                    stop=(m == n_hidden - 1),
+                    stop=(m == N_TILES - 1),
                 )
-            if 1 <= j < BLOCKS - 1:
+            if with_chunks:
                 regroup_gw(nc.vector.tensor_copy, vector_chunk, 0, DPB)
-                regroup_gw(nc.scalar.copy, scalar_chunk, 0, PIECE)
-            if j + 2 < BLOCKS:
-                quantise_w1(j + 2)
-            if j + 4 < BLOCKS:
-                quantise_hid0(j + 4)
-            if 1 <= j < BLOCKS - 1:
-                regroup_gw(nc.scalar.copy, scalar_chunk, PIECE, DPB)
+                regroup_gw(nc.scalar.copy, scalar_chunk, 0, DPB)
+            if j + W1_AHEAD < BLOCKS:
+                quantise_w1(j + W1_AHEAD)
+            if j + HID_AHEAD < BLOCKS:
+                quantise_hid0(j + HID_AHEAD)
+            if with_chunks:
                 quantise_gw(vector_chunk)
-        for q in range(VECTOR_WAIT_PIECES):
-            regroup_gw(
-                nc.vector.tensor_copy, EARLY_CHUNKS + q // 2, (q % 2) * PIECE, (q % 2 + 1) * PIECE
-            )
 
+        for chunk in range(EARLY_CHUNKS, FIRST_LATE_CHUNK):
+            regroup_gw(nc.vector.tensor_copy, chunk, 0, DPB)
         rms = const.tile([P, BATCH], F32)
         nc.scalar.activation(out=rms[:], in_=mean_ps[:], func=ACT.Sqrt, bias=eps[:, 0:1])
         rstd = const.tile([P, BATCH], F32)
         nc.vector.reciprocal(out=rstd[:], in_=rms[:])
-        late_quantise(2)
+        quantise_gw(EARLY_CHUNKS)
 
-        h_codes = keep.tile([P, BLOCKS, BATCH], U32, align_bytes=64)
-        h_scales = keep.tile([P, BLOCKS, BATCH], U8, align_bytes=64)
         h_grouped = {}
 
         def quantise_h(j):
@@ -316,19 +333,17 @@ def tile_deter_pb_kernel(tc, hid0, deter, hw1, hb1, hg1, gw, gb, out):
                 in_=h_grouped[j][:].rearrange("p w t -> p (w t)"),
             )
 
-        for half in range(HALVES):
-            u_tiles[half] = hidden_matmuls(half)
+        hidden_matmuls(0)
         for j in range(BLOCKS):
             if j + 1 < BLOCKS:
-                for half in range(HALVES):
-                    u_tiles[(j + 1) * HALVES + half] = hidden_matmuls((j + 1) * HALVES + half)
+                hidden_matmuls(j + 1)
             h_rows = stage.tile([P, PACK, BATCH], BF16)
             for t in range(FEAT_TILES):
                 m = j * FEAT_TILES + t
-                normed = stage.tile([P, BATCH], F32, tag="f32_tile", bufs=8)
+                normed = stage.tile([P, BATCH], F32, tag="f32_tile", bufs=F32_TILE_BUFS)
                 nc.vector.scalar_tensor_tensor(
                     out=normed[:],
-                    in0=u_tiles[m // 2][:, m % 2, :],
+                    in0=u_tile(m),
                     scalar=hb_cols[:, m : m + 1],
                     in1=rstd[:],
                     op0=ALU.add,
@@ -337,13 +352,11 @@ def tile_deter_pb_kernel(tc, hid0, deter, hw1, hb1, hg1, gw, gb, out):
                 nc.scalar.activation(
                     out=h_rows[:, t, :], in_=normed[:], func=ACT.Silu, scale=hg_cols[:, m : m + 1]
                 )
-            late_piece(VECTOR_WAIT_PIECES + j, nc.vector.tensor_copy)
-            late_quantise(VECTOR_WAIT_PIECES + j)
+            late_piece(j, nc.vector.tensor_copy)
+            late_quantise(j)
             if j >= 1:
                 quantise_h(j - 1)
-            h_grouped[j] = stage.tile(
-                [P, BATCH, PACK], BF16, name="h_grouped", bufs=1, align_bytes=64
-            )
+            h_grouped[j] = stage.tile([P, BATCH, PACK], BF16, name="h_grouped", bufs=1, align_bytes=64)
             regroup(gpsimd_copy, h_grouped[j][:], h_rows[:])
 
         out_view = out.rearrange(batch_major, p=P)
@@ -354,15 +367,17 @@ def tile_deter_pb_kernel(tc, hid0, deter, hw1, hb1, hg1, gw, gb, out):
         mix = {}
         mixT = {}
 
+        def unit_tile(name, bufs):
+            return stage.tile([P, TILES_PER_UNIT, BATCH], F32, name=name, bufs=bufs)
+
         def gate_matmuls(unit):
-            j, half = divmod(unit, HALVES)
+            j = unit // UNITS_PER_BLOCK
             for gate in (RESET, UPDATE, CAND):
-                acc = psum.tile([P, 2, BATCH], F32, tag="mm", bufs=5)
-                gate_ps[unit, gate] = acc
-                for s in range(2):
-                    first = gate * DPB + (2 * half + s) * P
+                gate_ps[unit, gate] = psum_tile([P, TILES_PER_UNIT, BATCH], F32, "mm")
+                for s in range(TILES_PER_UNIT):
+                    first = gate * DPB + (unit * TILES_PER_UNIT + s) * P - j * DPB
                     nc.tensor.matmul_mx(
-                        out=acc[:, s, :],
+                        out=gate_ps[unit, gate][:, s, :],
                         lhsT=gw_codes[:, j, first : first + P].bitcast(FP8X4),
                         lhsT_scale=gw_scales[:, j, first : first + P],
                         rhs=h_codes[:, j, :].bitcast(FP8X4),
@@ -372,9 +387,9 @@ def tile_deter_pb_kernel(tc, hid0, deter, hw1, hb1, hg1, gw, gb, out):
                     )
 
         def transpose_deter(unit):
-            deterT[unit] = psum.tile([P, 2, BATCH], BF16, name="deterT_ps", tag="inT", bufs=2)
-            for s in range(2):
-                first = (unit * 2 + s) * P
+            deterT[unit] = psum_tile([P, TILES_PER_UNIT, BATCH], BF16, "inT")
+            for s in range(TILES_PER_UNIT):
+                first = (unit * TILES_PER_UNIT + s) * P
                 for bt in range(BATCH_TILES):
                     nc.tensor.transpose(
                         deterT[unit][:, s, bt * P : (bt + 1) * P],
@@ -382,33 +397,36 @@ def tile_deter_pb_kernel(tc, hid0, deter, hw1, hb1, hg1, gw, gb, out):
                         ident_bf16[:],
                     )
 
+        def gate_bias(unit, gate, s):
+            j, t = divmod(unit * TILES_PER_UNIT + s, FEAT_TILES)
+            return gb_cols[:, j, gate, t : t + 1]
+
         def sigmoids(unit):
-            j, half = divmod(unit, HALVES)
-            reset[unit] = stage.tile([P, 2, BATCH], F32, name="reset")
-            update[unit] = stage.tile([P, 2, BATCH], F32, name="update", bufs=3)
+            reset[unit] = unit_tile("reset", STAGE_BUFS)
+            update[unit] = unit_tile("update", STEPS_ALIVE)
             for gate, result in ((RESET, reset[unit]), (UPDATE, update[unit])):
-                for s in range(2):
-                    t = 2 * half + s
+                for s in range(TILES_PER_UNIT):
                     nc.scalar.activation(
                         out=result[:, s, :],
                         in_=gate_ps[unit, gate][:, s, :],
                         func=ACT.Sigmoid,
-                        bias=gb_cols[:, j, gate, t : t + 1],
+                        bias=gate_bias(unit, gate, s),
                     )
 
         def reset_candidate(unit):
-            j, half = divmod(unit, HALVES)
-            mix[unit] = stage.tile([P, 2, BATCH], F32, name="mix", bufs=3)
-            for s in range(2):
-                t = 2 * half + s
+            mix[unit] = unit_tile("mix", STEPS_ALIVE)
+            for s in range(TILES_PER_UNIT):
                 nc.vector.scalar_tensor_tensor(
                     out=mix[unit][:, s, :],
                     in0=gate_ps[unit, CAND][:, s, :],
-                    scalar=gb_cols[:, j, CAND, t : t + 1],
+                    scalar=gate_bias(unit, CAND, s),
                     in1=reset[unit][:, s, :],
                     op0=ALU.add,
                     op1=ALU.mult,
                 )
+
+        def candidate(unit):
+            nc.scalar.activation(out=mix[unit][:], in_=mix[unit][:], func=ACT.Tanh)
 
         def mix_state(unit, multiplier):
             nc.vector.tensor_tensor(
@@ -419,8 +437,8 @@ def tile_deter_pb_kernel(tc, hid0, deter, hw1, hb1, hg1, gw, gb, out):
             )
 
         def transpose_mix(unit, tag):
-            mixT[unit] = psum.tile([P, BATCH_TILES, 2 * P], F32, name="mixT_ps", tag=tag, bufs=PSUM_BUFS[tag])
-            for s in range(2):
+            mixT[unit] = psum_tile([P, BATCH_TILES, UNIT_COLS], F32, tag)
+            for s in range(TILES_PER_UNIT):
                 for bt in range(BATCH_TILES):
                     nc.tensor.transpose(
                         mixT[unit][:, bt, s * P : (s + 1) * P],
@@ -429,8 +447,8 @@ def tile_deter_pb_kernel(tc, hid0, deter, hw1, hb1, hg1, gw, gb, out):
                     )
 
         def finish(unit):
-            cols = slice(unit * 2 * P, (unit + 1) * 2 * P)
-            new_state = stage.tile([P, BATCH_TILES, 2 * P], F32, bufs=3)
+            cols = slice(unit * UNIT_COLS, (unit + 1) * UNIT_COLS)
+            new_state = stage.tile([P, BATCH_TILES, UNIT_COLS], F32, bufs=STORE_BUFS)
             nc.vector.tensor_tensor(
                 out=new_state[:], in0=mixT[unit][:], in1=deter_sb[:, :, cols], op=ALU.add
             )
@@ -443,7 +461,7 @@ def tile_deter_pb_kernel(tc, hid0, deter, hw1, hb1, hg1, gw, gb, out):
             if step + 1 < UNITS:
                 gate_matmuls(step + 1)
             if step >= 1:
-                nc.scalar.activation(out=mix[step - 1][:], in_=mix[step - 1][:], func=ACT.Tanh)
+                candidate(step - 1)
             reset_candidate(step)
             if step >= 3:
                 finish(step - 3)
@@ -451,14 +469,15 @@ def tile_deter_pb_kernel(tc, hid0, deter, hw1, hb1, hg1, gw, gb, out):
                 transpose_mix(step - 2, "outT")
             if step == 0:
                 quantise_h(BLOCKS - 1)
-            late_piece(VECTOR_WAIT_PIECES + BLOCKS + step, gpsimd_copy)
-            late_quantise(VECTOR_WAIT_PIECES + BLOCKS + step)
+            late_piece(BLOCKS + step, gpsimd_copy)
+            late_quantise(BLOCKS + step)
             if step >= 1:
                 mix_state(step - 1, nc.gpsimd)
             if step + 1 < UNITS:
                 transpose_deter(step + 1)
+
         last = UNITS - 1
-        nc.scalar.activation(out=mix[last][:], in_=mix[last][:], func=ACT.Tanh)
+        candidate(last)
         finish(last - 2)
         transpose_mix(last - 1, "outT")
         mix_state(last, nc.vector)

@@ -308,12 +308,13 @@ def tile_deter_pb_kernel(tc, hid0, deter, hw1, hb1, hg1, gw, gb, out):
                 )
             if with_chunks:
                 regroup_gw(nc.vector.tensor_copy, vector_chunk, 0, DPB)
-                regroup_gw(nc.scalar.copy, scalar_chunk, 0, DPB)
+                regroup_gw(nc.scalar.copy, scalar_chunk, 0, PIECE)
             if j + W1_AHEAD < BLOCKS:
                 quantise_w1(j + W1_AHEAD)
             if j + HID_AHEAD < BLOCKS:
                 quantise_hid0(j + HID_AHEAD)
             if with_chunks:
+                regroup_gw(nc.scalar.copy, scalar_chunk, PIECE, DPB)
                 quantise_gw(vector_chunk)
 
         for chunk in range(EARLY_CHUNKS, FIRST_LATE_CHUNK):

@@ -35,6 +35,8 @@ PIECE = DPB // 2
 EARLY_CHUNKS = 2 * (BLOCKS - 2)
 WAIT_CHUNKS = 2
 FIRST_LATE_CHUNK = EARLY_CHUNKS + WAIT_CHUNKS
+LATE_CHUNKS = CHUNKS - FIRST_LATE_CHUNK
+LATE_SPLIT = 3 * DPB // 4
 
 PAIR = 2
 PAIRS = BLOCKS // PAIR
@@ -217,16 +219,9 @@ def tile_deter_pb_kernel(tc, hid0, deter, hw1, hb1, hg1, gw, gb, out):
                 out=out, in0=in_, scalar1=1.0, scalar2=0.0, op0=ALU.mult, op1=ALU.add
             )
 
-        def late_piece(q, odd_copy):
-            chunk, half = divmod(q, 2)
-            copy = nc.scalar.copy if half == 0 else odd_copy
-            if FIRST_LATE_CHUNK + chunk < CHUNKS:
-                regroup_gw(copy, FIRST_LATE_CHUNK + chunk, half * PIECE, (half + 1) * PIECE)
-
-        def late_quantise(q):
-            chunk, half = divmod(q, 2)
-            if half == 0 and FIRST_LATE_CHUNK + chunk - 1 < CHUNKS:
-                quantise_gw(FIRST_LATE_CHUNK + chunk - 1)
+        def late_chunks(j):
+            first = FIRST_LATE_CHUNK + j * LATE_CHUNKS // BLOCKS
+            return range(first, FIRST_LATE_CHUNK + (j + 1) * LATE_CHUNKS // BLOCKS)
 
         u_ps = {}
 
@@ -353,10 +348,15 @@ def tile_deter_pb_kernel(tc, hid0, deter, hw1, hb1, hg1, gw, gb, out):
                 nc.scalar.activation(
                     out=h_rows[:, t, :], in_=normed[:], func=ACT.Silu, scale=hg_cols[:, m : m + 1]
                 )
-            late_piece(j, nc.vector.tensor_copy)
-            late_quantise(j)
-            if j >= 1:
+            if j == 0:
+                quantise_gw(FIRST_LATE_CHUNK - 1)
+            else:
+                for chunk in late_chunks(j - 1):
+                    quantise_gw(chunk)
                 quantise_h(j - 1)
+            for chunk in late_chunks(j):
+                regroup_gw(nc.scalar.copy, chunk, 0, LATE_SPLIT)
+                regroup_gw(nc.vector.tensor_copy, chunk, LATE_SPLIT, DPB)
             h_grouped[j] = stage.tile([P, BATCH, PACK], BF16, name="h_grouped", bufs=1, align_bytes=64)
             regroup(gpsimd_copy, h_grouped[j][:], h_rows[:])
 
@@ -470,8 +470,9 @@ def tile_deter_pb_kernel(tc, hid0, deter, hw1, hb1, hg1, gw, gb, out):
                 transpose_mix(step - 2, "outT")
             if step == 0:
                 quantise_h(BLOCKS - 1)
-            late_piece(BLOCKS + step, gpsimd_copy)
-            late_quantise(BLOCKS + step)
+            if step == 0:
+                for chunk in late_chunks(BLOCKS - 1):
+                    quantise_gw(chunk)
             if step >= 1:
                 mix_state(step - 1, nc.gpsimd)
             if step + 1 < UNITS:

@@ -35,8 +35,16 @@ PIECE = DPB // 2
 EARLY_CHUNKS = 2 * (BLOCKS - 2)
 WAIT_CHUNKS = 2
 FIRST_LATE_CHUNK = EARLY_CHUNKS + WAIT_CHUNKS
-LATE_CHUNKS = CHUNKS - FIRST_LATE_CHUNK
-LATE_SPLIT = 3 * DPB // 4
+W1_BUFS = 4
+W1_SPLIT = 512
+P1_SPLIT = 256
+P2_SPLIT = 256
+P1 = [0, 1, 1, 1, 1, 1, 1, 2]
+WAIT = 2
+P2_ROUNDS = 7
+G_CHUNKS = 0
+G_PIECES = 2
+LOADS_AFTER_W1 = {2: [("g", 1)], 3: [("h", 3), ("g", 2)]}
 
 PAIR = 2
 PAIRS = BLOCKS // PAIR
@@ -110,15 +118,12 @@ def tile_deter_pb_kernel(tc, hid0, deter, hw1, hb1, hg1, gw, gb, out):
                 out=hid_sb[:, pair, :, :], in_=hid0.rearrange(batch_major, p=P)[:, :, cols]
             )
 
-        def load_w1_pair(pair):
-            w1_rows[pair] = wraw.tile(
-                [P, PAIR, PACK, DPB], BF16, name="w1_rows", bufs=W1_PAIRS_AHEAD
+        def load_w1(j):
+            w1_rows[j] = wraw.tile([P, PACK, DPB], BF16, name="w1_rows", bufs=W1_BUFS)
+            nc.sync.dma_start(
+                out=w1_rows[j][:].rearrange("p (u e) n -> p u (e n)", e=2),
+                in_=hw1[j].rearrange("(u p e) n -> p u (e n)", u=WORDS, e=2),
             )
-            for i in range(PAIR):
-                nc.sync.dma_start(
-                    out=w1_rows[pair][:, i, :, :].rearrange("p (u e) n -> p u (e n)", e=2),
-                    in_=hw1[PAIR * pair + i].rearrange("(u p e) n -> p u (e n)", u=WORDS, e=2),
-                )
 
         def load_gw(block):
             gw_rows[block] = wraw.tile(
@@ -126,20 +131,21 @@ def tile_deter_pb_kernel(tc, hid0, deter, hw1, hb1, hg1, gw, gb, out):
             )
             nc.sync.dma_start(out=gw_rows[block][:], in_=gw[block].rearrange("(t p) n -> p t n", p=P))
 
-        load_hid0(0)
-        load_w1_pair(0)
-        nc.sync.dma_start(out=hidden_rows[0:N_TILES, :], in_=hb1.rearrange("(m p) -> m p", p=P))
-        nc.sync.dma_start(
+        nc.scalar.dma_start(out=hidden_rows[0:N_TILES, :], in_=hb1.rearrange("(m p) -> m p", p=P))
+        nc.scalar.dma_start(
             out=hidden_rows[N_TILES : 2 * N_TILES, :], in_=hg1.rearrange("(m p) -> m p", p=P)
         )
-        nc.sync.dma_start(
+        nc.scalar.dma_start(
             out=gate_rows[0 : GATES * N_TILES, :], in_=gb.rearrange("(m p) -> m p", p=P)
         )
+        load_w1(0)
+        load_hid0(0)
+        load_w1(1)
+        load_w1(2)
         load_hid0(1)
-        load_w1_pair(1)
-        load_hid0(2)
-        load_hid0(3)
+        load_w1(3)
         load_gw(0)
+        load_hid0(2)
 
         hid_words = hid_sb[:].bitcast(F32)
         words_per_block = DPB // 2
@@ -157,16 +163,20 @@ def tile_deter_pb_kernel(tc, hid0, deter, hw1, hb1, hg1, gw, gb, out):
                         ident_f32[:],
                     )
 
-        def quantise_hid0(j):
-            hid_grouped = stage.tile([P, BATCH * PACK], BF16, align_bytes=64)
+        hid_grouped = {}
+
+        def copy_hid0(j):
+            hid_grouped[j] = stage.tile([P, BATCH * PACK], BF16, name="hid_grouped", align_bytes=64)
             nc.scalar.copy(
-                out=hid_grouped[:].bitcast(F32).rearrange("p (b u) -> p b u", u=WORDS),
+                out=hid_grouped[j][:].bitcast(F32).rearrange("p (b u) -> p b u", u=WORDS),
                 in_=hidT[j][:].rearrange("p u b -> p b u"),
             )
+
+        def quantise_hid0(j):
             nc.vector.quantize_mx(
                 out=hid_codes[:, j, :].bitcast(FP8X4),
                 scales=hid_scales[:, j, :],
-                in_=hid_grouped[:],
+                in_=hid_grouped[j][:],
             )
 
         def grouped_tile():
@@ -176,13 +186,16 @@ def tile_deter_pb_kernel(tc, hid0, deter, hw1, hb1, hg1, gw, gb, out):
 
         w1_grouped = {}
 
-        def regroup_w1(copy, j):
-            pair, i = divmod(j, PAIR)
+        def regroup_w1(j):
             w1_grouped[j] = grouped_tile()
-            regroup(copy, w1_grouped[j][:], w1_rows[pair][:, i, :, :])
-            if i == PAIR - 1 and pair + W1_PAIRS_AHEAD < PAIRS:
-                load_w1_pair(pair + W1_PAIRS_AHEAD)
-                load_gw(pair + 1)
+            for copy, lo, hi in ((nc.vector.tensor_copy, 0, W1_SPLIT), (nc.scalar.copy, W1_SPLIT, DPB)):
+                if lo < hi:
+                    regroup(copy, w1_grouped[j][:, lo:hi, :], w1_rows[j][:, :, lo:hi])
+            if j + W1_BUFS < BLOCKS:
+                load_w1(j + W1_BUFS)
+            if j in LOADS_AFTER_W1:
+                for kind, n in LOADS_AFTER_W1[j]:
+                    (load_hid0 if kind == "h" else load_gw)(n)
 
         def quantise_w1(j):
             nc.vector.quantize_mx(
@@ -195,14 +208,18 @@ def tile_deter_pb_kernel(tc, hid0, deter, hw1, hb1, hg1, gw, gb, out):
 
         def regroup_gw(copy, chunk, lo, hi):
             block, gate = divmod(chunk, GATES)
-            if lo == 0:
+            if chunk not in gw_grouped:
                 gw_grouped[chunk] = grouped_tile()
-            regroup(
-                copy,
-                gw_grouped[chunk][:, lo:hi, :],
-                gw_rows[block][:, :, gate * DPB + lo : gate * DPB + hi],
-            )
-            if gate == GATES - 1 and hi == DPB and block + GW_AHEAD < BLOCKS:
+            if lo < hi:
+                regroup(
+                    copy,
+                    gw_grouped[chunk][:, lo:hi, :],
+                    gw_rows[block][:, :, gate * DPB + lo : gate * DPB + hi],
+                )
+
+        def free_gw(chunk):
+            block, gate = divmod(chunk, GATES)
+            if gate == GATES - 1 and block + GW_AHEAD < BLOCKS:
                 load_gw(block + GW_AHEAD)
 
         def quantise_gw(chunk):
@@ -214,14 +231,15 @@ def tile_deter_pb_kernel(tc, hid0, deter, hw1, hb1, hg1, gw, gb, out):
                 in_=gw_grouped[chunk][:].rearrange("p w t -> p (w t)"),
             )
 
+        def share(chunk, split):
+            regroup_gw(nc.vector.tensor_copy, chunk, 0, split)
+            regroup_gw(nc.scalar.copy, chunk, split, DPB)
+            free_gw(chunk)
+
         def gpsimd_copy(out, in_):
             nc.gpsimd.tensor_scalar(
                 out=out, in0=in_, scalar1=1.0, scalar2=0.0, op0=ALU.mult, op1=ALU.add
             )
-
-        def late_chunks(j):
-            first = FIRST_LATE_CHUNK + j * LATE_CHUNKS // BLOCKS
-            return range(first, FIRST_LATE_CHUNK + (j + 1) * LATE_CHUNKS // BLOCKS)
 
         u_ps = {}
 
@@ -243,52 +261,43 @@ def tile_deter_pb_kernel(tc, hid0, deter, hw1, hb1, hg1, gw, gb, out):
         def u_tile(m):
             return u_ps[m // TILES_PER_UNIT][:, m % TILES_PER_UNIT, :]
 
-        for j in range(PAIR):
-            transpose_hid0(j)
-            quantise_hid0(j)
-        regroup_w1(nc.vector.tensor_copy, 0)
-        regroup_w1(nc.scalar.copy, 1)
+        def table(func):
+            nc.scalar.activation(out=scrap[:], in_=eps[:], func=func)
 
+        scrap = const.tile([P, 1], F32)
+        table(ACT.Sqrt)
+        regroup_w1(0)
+        transpose_hid0(0)
+        transpose_hid0(1)
+        copy_hid0(0)
+        quantise_w1(0)
+        copy_hid0(1)
         hidden_cols_ps = psum_tile([P, P], BF16, "mm")
         nc.tensor.transpose(hidden_cols_ps[:], hidden_rows[:], ident_bf16[:])
         hidden_cols = const.tile([P, 2 * N_TILES], F32)
+        gate_cols_ps = psum_tile([P, P], BF16, "mm")
+        nc.tensor.transpose(gate_cols_ps[:], gate_rows[:], ident_bf16[:])
+        quantise_hid0(0)
         nc.vector.tensor_copy(out=hidden_cols[:], in_=hidden_cols_ps[:, 0 : 2 * N_TILES])
         hb_cols = hidden_cols[:, 0:N_TILES]
         hg_cols = hidden_cols[:, N_TILES : 2 * N_TILES]
-        gate_cols_ps = psum_tile([P, P], BF16, "mm")
-        nc.tensor.transpose(gate_cols_ps[:], gate_rows[:], ident_bf16[:])
         gb_cols = const.tile([P, BLOCKS, GATES, FEAT_TILES], F32)
+        hidden_matmuls(0)
+        regroup_w1(1)
         nc.vector.tensor_copy(
             out=gb_cols[:].rearrange("p j g t -> p (j g t)"), in_=gate_cols_ps[:, 0 : GATES * N_TILES]
         )
-        nc.vector.tensor_scalar_add(
-            out=gb_cols[:, :, UPDATE, :], in0=gb_cols[:, :, UPDATE, :], scalar1=-1.0
-        )
-
-        for j in range(PAIR, HID_AHEAD):
-            transpose_hid0(j)
-        quantise_w1(0)
-        hidden_matmuls(0)
-        for j in range(PAIR, HID_AHEAD):
-            quantise_hid0(j)
-        quantise_w1(1)
 
         mean_ps = psum_tile([P, BATCH], F32, "outT")
+        done = 0
+        ready = []
         for j in range(BLOCKS):
-            with_chunks = 1 <= j < BLOCKS - 1
-            vector_chunk = 2 * (j - 1)
-            scalar_chunk = vector_chunk + 1
-            if j >= 2:
-                quantise_gw(scalar_chunk - 2)
-            if j + W1_AHEAD < BLOCKS:
-                regroup_w1(nc.vector.tensor_copy, j + W1_AHEAD)
             if j + 1 < BLOCKS:
+                quantise_hid0(j + 1)
+                quantise_w1(j + 1)
                 hidden_matmuls(j + 1)
-            if j + HID_AHEAD < BLOCKS:
-                transpose_hid0(j + HID_AHEAD)
-            if j + HID_AHEAD == BLOCKS - 1:
-                deter_sb = acts.tile([P, BATCH_TILES, DETER], BF16, tag="acts")
-                nc.sync.dma_start(out=deter_sb[:], in_=deter.rearrange(batch_major, p=P))
+            if j + 2 < BLOCKS:
+                transpose_hid0(j + 2)
             for m in range(j * FEAT_TILES, (j + 1) * FEAT_TILES):
                 squares = stage.tile([P, BATCH], F32, tag="f32_tile", bufs=F32_TILE_BUFS)
                 nc.scalar.activation(
@@ -301,25 +310,41 @@ def tile_deter_pb_kernel(tc, hid0, deter, hw1, hb1, hg1, gw, gb, out):
                     start=(m == 0),
                     stop=(m == N_TILES - 1),
                 )
-            if with_chunks:
-                regroup_gw(nc.vector.tensor_copy, vector_chunk, 0, DPB)
-                regroup_gw(nc.scalar.copy, scalar_chunk, 0, PIECE)
-            if j + W1_AHEAD < BLOCKS:
-                quantise_w1(j + W1_AHEAD)
-            if j + HID_AHEAD < BLOCKS:
-                quantise_hid0(j + HID_AHEAD)
-            if with_chunks:
-                regroup_gw(nc.scalar.copy, scalar_chunk, PIECE, DPB)
-                quantise_gw(vector_chunk)
-
-        for chunk in range(EARLY_CHUNKS, FIRST_LATE_CHUNK):
-            regroup_gw(nc.vector.tensor_copy, chunk, 0, DPB)
+            if j + 2 < BLOCKS:
+                regroup_w1(j + 2)
+            if j == 5:
+                deter_sb = acts.tile([P, BATCH_TILES, DETER], BF16, tag="acts")
+            for chunk in ready:
+                quantise_gw(chunk)
+            ready = []
+            for n in range(P1[j]):
+                share(done, P1_SPLIT)
+                ready.append(done)
+                done += 1
+            if j + 2 < BLOCKS:
+                copy_hid0(j + 2)
+        if True:
+            nc.sync.dma_start(out=deter_sb[:], in_=deter.rearrange(batch_major, p=P))
+        nc.vector.tensor_scalar_add(
+            out=gb_cols[:, :, UPDATE, :], in0=gb_cols[:, :, UPDATE, :], scalar1=-1.0
+        )
+        for chunk in ready:
+            quantise_gw(chunk)
+        ready = []
+        hidden_matmuls(0)
+        table(ACT.Sqrt)
+        for n in range(WAIT):
+            regroup_gw(nc.vector.tensor_copy, done, 0, DPB)
+            free_gw(done)
+            ready.append(done)
+            done += 1
         rms = const.tile([P, BATCH], F32)
         nc.scalar.activation(out=rms[:], in_=mean_ps[:], func=ACT.Sqrt, bias=eps[:, 0:1])
+        table(ACT.Silu)
         rstd = const.tile([P, BATCH], F32)
         nc.vector.reciprocal(out=rstd[:], in_=rms[:])
-        quantise_gw(EARLY_CHUNKS)
 
+        rest = CHUNKS - done - G_CHUNKS
         h_grouped = {}
 
         def quantise_h(j):
@@ -329,7 +354,6 @@ def tile_deter_pb_kernel(tc, hid0, deter, hw1, hb1, hg1, gw, gb, out):
                 in_=h_grouped[j][:].rearrange("p w t -> p (w t)"),
             )
 
-        hidden_matmuls(0)
         for j in range(BLOCKS):
             if j + 1 < BLOCKS:
                 hidden_matmuls(j + 1)
@@ -348,17 +372,18 @@ def tile_deter_pb_kernel(tc, hid0, deter, hw1, hb1, hg1, gw, gb, out):
                 nc.scalar.activation(
                     out=h_rows[:, t, :], in_=normed[:], func=ACT.Silu, scale=hg_cols[:, m : m + 1]
                 )
-            if j == 0:
-                quantise_gw(FIRST_LATE_CHUNK - 1)
-            else:
-                for chunk in late_chunks(j - 1):
-                    quantise_gw(chunk)
+            for chunk in ready:
+                quantise_gw(chunk)
+            ready = []
+            for n in range((j + 1) * rest // P2_ROUNDS - j * rest // P2_ROUNDS if j < P2_ROUNDS else 0):
+                share(done, P2_SPLIT)
+                ready.append(done)
+                done += 1
+            if j >= 1:
                 quantise_h(j - 1)
-            for chunk in late_chunks(j):
-                regroup_gw(nc.scalar.copy, chunk, 0, LATE_SPLIT)
-                regroup_gw(nc.vector.tensor_copy, chunk, LATE_SPLIT, DPB)
             h_grouped[j] = stage.tile([P, BATCH, PACK], BF16, name="h_grouped", bufs=1, align_bytes=64)
             regroup(gpsimd_copy, h_grouped[j][:], h_rows[:])
+        table(ACT.Sigmoid)
 
         out_view = out.rearrange(batch_major, p=P)
         gate_ps = {}
@@ -470,9 +495,17 @@ def tile_deter_pb_kernel(tc, hid0, deter, hw1, hb1, hg1, gw, gb, out):
                 transpose_mix(step - 2, "outT")
             if step == 0:
                 quantise_h(BLOCKS - 1)
-            if step == 0:
-                for chunk in late_chunks(BLOCKS - 1):
+                for chunk in ready:
                     quantise_gw(chunk)
+            if G_CHUNKS and step >= 0:
+                piece = step - 1
+                chunk = CHUNKS - G_CHUNKS + piece // G_PIECES
+                if piece >= 0 and chunk < CHUNKS:
+                    w = DPB // G_PIECES
+                    q = piece % G_PIECES
+                    regroup_gw(gpsimd_copy, chunk, q * w, q * w + w)
+                if piece > 0 and piece % G_PIECES == 0 and chunk <= CHUNKS:
+                    quantise_gw(chunk - 1)
             if step >= 1:
                 mix_state(step - 1, nc.gpsimd)
             if step + 1 < UNITS:

@@ -37,12 +37,14 @@ WAIT_CHUNKS = 2
 FIRST_LATE_CHUNK = EARLY_CHUNKS + WAIT_CHUNKS
 W1_BUFS = 4
 W1_SPLIT = 512
-P1_SPLIT = 256
-P2_SPLIT = 256
-P1 = [0, 1, 1, 1, 1, 1, 1, 2]
-WAIT = 2
+P1_SPLIT = 224
+P2_SPLIT = 224
+P1 = [0, 1, 1, 1, 1, 1, 1, 1]
+P1V = [0, 0, 0, 0, 0, 0, 1, 1]
+WAIT = 1
 P2_ROUNDS = 7
 G_CHUNKS = 0
+LASTV = 1
 G_PIECES = 2
 LOADS_AFTER_W1 = {2: [("g", 1)], 3: [("h", 3), ("g", 2)]}
 
@@ -57,7 +59,7 @@ PSUM_BUFS = {"mm": 5, "inT": 2, "outT": 1}
 STAGE_BUFS = 2
 GROUPED_BUFS = 4
 F32_TILE_BUFS = 2 * FEAT_TILES
-STEPS_ALIVE = 3
+STEPS_ALIVE = 4
 STORE_BUFS = 3
 
 FLOPS = 2 * BATCH * DPB * (DPB + GATES * DPB) * BLOCKS
@@ -141,8 +143,8 @@ def tile_deter_pb_kernel(tc, hid0, deter, hw1, hb1, hg1, gw, gb, out):
         load_w1(0)
         load_hid0(0)
         load_w1(1)
-        load_w1(2)
         load_hid0(1)
+        load_w1(2)
         load_w1(3)
         load_gw(0)
         load_hid0(2)
@@ -292,12 +294,12 @@ def tile_deter_pb_kernel(tc, hid0, deter, hw1, hb1, hg1, gw, gb, out):
         done = 0
         ready = []
         for j in range(BLOCKS):
+            if j + 2 < BLOCKS:
+                transpose_hid0(j + 2)
             if j + 1 < BLOCKS:
                 quantise_hid0(j + 1)
                 quantise_w1(j + 1)
                 hidden_matmuls(j + 1)
-            if j + 2 < BLOCKS:
-                transpose_hid0(j + 2)
             for m in range(j * FEAT_TILES, (j + 1) * FEAT_TILES):
                 squares = stage.tile([P, BATCH], F32, tag="f32_tile", bufs=F32_TILE_BUFS)
                 nc.scalar.activation(
@@ -319,6 +321,10 @@ def tile_deter_pb_kernel(tc, hid0, deter, hw1, hb1, hg1, gw, gb, out):
             ready = []
             for n in range(P1[j]):
                 share(done, P1_SPLIT)
+                ready.append(done)
+                done += 1
+            for n in range(P1V[j]):
+                share(done, DPB)
                 ready.append(done)
                 done += 1
             if j + 2 < BLOCKS:
@@ -344,7 +350,7 @@ def tile_deter_pb_kernel(tc, hid0, deter, hw1, hb1, hg1, gw, gb, out):
         rstd = const.tile([P, BATCH], F32)
         nc.vector.reciprocal(out=rstd[:], in_=rms[:])
 
-        rest = CHUNKS - done - G_CHUNKS
+        rest = CHUNKS - done - G_CHUNKS - LASTV
         h_grouped = {}
 
         def quantise_h(j):
@@ -375,12 +381,20 @@ def tile_deter_pb_kernel(tc, hid0, deter, hw1, hb1, hg1, gw, gb, out):
             for chunk in ready:
                 quantise_gw(chunk)
             ready = []
-            for n in range((j + 1) * rest // P2_ROUNDS - j * rest // P2_ROUNDS if j < P2_ROUNDS else 0):
+            count = (j + 1) * rest // P2_ROUNDS - j * rest // P2_ROUNDS if j < P2_ROUNDS else 0
+            if j >= 1 and count == 0:
+                quantise_h(j - 1)
+            for n in range(count):
+                if j >= 1 and n == count - 1:
+                    quantise_h(j - 1)
                 share(done, P2_SPLIT)
                 ready.append(done)
                 done += 1
-            if j >= 1:
-                quantise_h(j - 1)
+            if j == BLOCKS - 1:
+                for n in range(LASTV):
+                    share(done, DPB)
+                    ready.append(done)
+                    done += 1
             h_grouped[j] = stage.tile([P, BATCH, PACK], BF16, name="h_grouped", bufs=1, align_bytes=64)
             regroup(gpsimd_copy, h_grouped[j][:], h_rows[:])
         table(ACT.Sigmoid)
@@ -481,11 +495,11 @@ def tile_deter_pb_kernel(tc, hid0, deter, hw1, hb1, hg1, gw, gb, out):
             nc.sync.dma_start(out=out_view[:, :, cols], in_=new_state[:])
 
         gate_matmuls(0)
-        transpose_deter(0)
         for step in range(UNITS):
             sigmoids(step)
             if step + 1 < UNITS:
                 gate_matmuls(step + 1)
+            transpose_deter(step)
             if step >= 1:
                 candidate(step - 1)
             reset_candidate(step)
@@ -508,8 +522,6 @@ def tile_deter_pb_kernel(tc, hid0, deter, hw1, hb1, hg1, gw, gb, out):
                     quantise_gw(chunk - 1)
             if step >= 1:
                 mix_state(step - 1, nc.gpsimd)
-            if step + 1 < UNITS:
-                transpose_deter(step + 1)
 
         last = UNITS - 1
         candidate(last)

@@ -36,17 +36,30 @@ EARLY_CHUNKS = 2 * (BLOCKS - 2)
 WAIT_CHUNKS = 2
 FIRST_LATE_CHUNK = EARLY_CHUNKS + WAIT_CHUNKS
 W1_BUFS = 4
-W1_SPLIT = 512
-P1_SPLIT = 224
+W1_LATE = [0, 0, 1, 0, 0, 0, 0, 0]
+W1_SPLITS = [384] * 4 + [512] * 4
+P1_SPLIT = 256
 P2_SPLIT = 224
-P1 = [0, 1, 1, 1, 1, 1, 1, 1]
-P1V = [0, 0, 0, 0, 0, 0, 1, 1]
-WAIT = 1
+P1 = [0, 2, 1, 1, 1, 1, 0, 2]
+P1V = [0, 0, 0, 0, 0, 0, 1, 0]
+WAIT = 0
+WAIT2 = 1
 P2_ROUNDS = 7
 G_CHUNKS = 0
 LASTV = 1
+H_STEP = 1
+GW_SPLIT = 1
+KEPT_BUFS = 3
+SEAM_SPLIT = 224
+SEAM_V = 1
+PE_ROUNDS = 0
+BANK_COLS = 256
+TR_AHEAD = 2
+COPY_FIRST = True
+HID_EARLY = False
+SEAM_Q = 3
 G_PIECES = 2
-LOADS_AFTER_W1 = {2: [("g", 1)], 3: [("h", 3), ("g", 2)]}
+LOADS_AFTER_W1 = {2: [('h', 3), ('g', 1)], 3: [('g', 2)]}
 
 PAIR = 2
 PAIRS = BLOCKS // PAIR
@@ -131,7 +144,14 @@ def tile_deter_pb_kernel(tc, hid0, deter, hw1, hb1, hg1, gw, gb, out):
             gw_rows[block] = wraw.tile(
                 [P, PACK, GATES * DPB], BF16, name="gw_rows", bufs=GW_AHEAD
             )
-            nc.sync.dma_start(out=gw_rows[block][:], in_=gw[block].rearrange("(t p) n -> p t n", p=P))
+            parts = GATES if block < GW_SPLIT else 1
+            width = GATES * DPB // parts
+            for part in range(parts):
+                cols = slice(part * width, (part + 1) * width)
+                nc.sync.dma_start(
+                    out=gw_rows[block][:, :, cols],
+                    in_=gw[block].rearrange("(t p) n -> p t n", p=P)[:, :, cols],
+                )
 
         nc.scalar.dma_start(out=hidden_rows[0:N_TILES, :], in_=hb1.rearrange("(m p) -> m p", p=P))
         nc.scalar.dma_start(
@@ -146,8 +166,11 @@ def tile_deter_pb_kernel(tc, hid0, deter, hw1, hb1, hg1, gw, gb, out):
         load_hid0(1)
         load_w1(2)
         load_w1(3)
+        if HID_EARLY:
+            load_hid0(2)
         load_gw(0)
-        load_hid0(2)
+        if not HID_EARLY:
+            load_hid0(2)
 
         hid_words = hid_sb[:].bitcast(F32)
         words_per_block = DPB // 2
@@ -190,7 +213,8 @@ def tile_deter_pb_kernel(tc, hid0, deter, hw1, hb1, hg1, gw, gb, out):
 
         def regroup_w1(j):
             w1_grouped[j] = grouped_tile()
-            for copy, lo, hi in ((nc.vector.tensor_copy, 0, W1_SPLIT), (nc.scalar.copy, W1_SPLIT, DPB)):
+            split = W1_SPLITS[j]
+            for copy, lo, hi in ((nc.vector.tensor_copy, 0, split), (nc.scalar.copy, split, DPB)):
                 if lo < hi:
                     regroup(copy, w1_grouped[j][:, lo:hi, :], w1_rows[j][:, :, lo:hi])
             if j + W1_BUFS < BLOCKS:
@@ -232,6 +256,28 @@ def tile_deter_pb_kernel(tc, hid0, deter, hw1, hb1, hg1, gw, gb, out):
                 scales=gw_scales[:, block, cols],
                 in_=gw_grouped[chunk][:].rearrange("p w t -> p (w t)"),
             )
+
+        def tensor_regroup(chunk):
+            block, gate = divmod(chunk, GATES)
+            gw_grouped[chunk] = grouped_tile()
+            banks = []
+            for lo in range(0, DPB, BANK_COLS):
+                bank = psum_tile([P, BANK_COLS, PACK], BF16, "inT")
+                for t in range(PACK):
+                    nc.tensor.matmul(
+                        out=bank[:, :, t],
+                        lhsT=ident_bf16[:],
+                        rhs=gw_rows[block][:, t, gate * DPB + lo : gate * DPB + lo + BANK_COLS],
+                        start=True,
+                        stop=True,
+                    )
+                banks.append((lo, bank))
+            free_gw(chunk)
+            return banks
+
+        def copy_banks(chunk, banks):
+            for lo, bank in banks:
+                nc.scalar.copy(out=gw_grouped[chunk][:, lo : lo + BANK_COLS, :], in_=bank[:])
 
         def share(chunk, split):
             regroup_gw(nc.vector.tensor_copy, chunk, 0, split)
@@ -294,8 +340,10 @@ def tile_deter_pb_kernel(tc, hid0, deter, hw1, hb1, hg1, gw, gb, out):
         done = 0
         ready = []
         for j in range(BLOCKS):
-            if j + 2 < BLOCKS:
-                transpose_hid0(j + 2)
+            if j == 0 and TR_AHEAD == 3:
+                transpose_hid0(2)
+            if j + TR_AHEAD < BLOCKS:
+                transpose_hid0(j + TR_AHEAD)
             if j + 1 < BLOCKS:
                 quantise_hid0(j + 1)
                 quantise_w1(j + 1)
@@ -312,13 +360,15 @@ def tile_deter_pb_kernel(tc, hid0, deter, hw1, hb1, hg1, gw, gb, out):
                     start=(m == 0),
                     stop=(m == N_TILES - 1),
                 )
-            if j + 2 < BLOCKS:
+            if j + 2 < BLOCKS and not W1_LATE[j]:
                 regroup_w1(j + 2)
-            if j == 5:
+            if j + TR_AHEAD == BLOCKS - 1:
                 deter_sb = acts.tile([P, BATCH_TILES, DETER], BF16, tag="acts")
             for chunk in ready:
                 quantise_gw(chunk)
             ready = []
+            if j + 2 < BLOCKS and COPY_FIRST:
+                copy_hid0(j + 2)
             for n in range(P1[j]):
                 share(done, P1_SPLIT)
                 ready.append(done)
@@ -327,30 +377,34 @@ def tile_deter_pb_kernel(tc, hid0, deter, hw1, hb1, hg1, gw, gb, out):
                 share(done, DPB)
                 ready.append(done)
                 done += 1
-            if j + 2 < BLOCKS:
+            if j + 2 < BLOCKS and W1_LATE[j]:
+                regroup_w1(j + 2)
+            if j + 2 < BLOCKS and not COPY_FIRST:
                 copy_hid0(j + 2)
         if True:
             nc.sync.dma_start(out=deter_sb[:], in_=deter.rearrange(batch_major, p=P))
         nc.vector.tensor_scalar_add(
             out=gb_cols[:, :, UPDATE, :], in0=gb_cols[:, :, UPDATE, :], scalar1=-1.0
         )
+        table(ACT.Sqrt)
         for chunk in ready:
             quantise_gw(chunk)
         ready = []
         hidden_matmuls(0)
-        table(ACT.Sqrt)
-        for n in range(WAIT):
-            regroup_gw(nc.vector.tensor_copy, done, 0, DPB)
-            free_gw(done)
+        for n in range(SEAM_V):
+            share(done, DPB)
             ready.append(done)
             done += 1
         rms = const.tile([P, BATCH], F32)
         nc.scalar.activation(out=rms[:], in_=mean_ps[:], func=ACT.Sqrt, bias=eps[:, 0:1])
+        share(done, SEAM_SPLIT)
+        ready.append(done)
+        done += 1
         table(ACT.Silu)
         rstd = const.tile([P, BATCH], F32)
         nc.vector.reciprocal(out=rstd[:], in_=rms[:])
 
-        rest = CHUNKS - done - G_CHUNKS - LASTV
+        rest = CHUNKS - done - G_CHUNKS - LASTV - PE_ROUNDS
         h_grouped = {}
 
         def quantise_h(j):
@@ -363,6 +417,11 @@ def tile_deter_pb_kernel(tc, hid0, deter, hw1, hb1, hg1, gw, gb, out):
         for j in range(BLOCKS):
             if j + 1 < BLOCKS:
                 hidden_matmuls(j + 1)
+            banks = []
+            by_tensor = done
+            if j < PE_ROUNDS:
+                done += 1
+                banks = tensor_regroup(by_tensor)
             h_rows = stage.tile([P, PACK, BATCH], BF16)
             for t in range(FEAT_TILES):
                 m = j * FEAT_TILES + t
@@ -381,6 +440,9 @@ def tile_deter_pb_kernel(tc, hid0, deter, hw1, hb1, hg1, gw, gb, out):
             for chunk in ready:
                 quantise_gw(chunk)
             ready = []
+            if banks:
+                copy_banks(by_tensor, banks)
+                ready.append(by_tensor)
             count = (j + 1) * rest // P2_ROUNDS - j * rest // P2_ROUNDS if j < P2_ROUNDS else 0
             if j >= 1 and count == 0:
                 quantise_h(j - 1)
@@ -401,7 +463,8 @@ def tile_deter_pb_kernel(tc, hid0, deter, hw1, hb1, hg1, gw, gb, out):
 
         out_view = out.rearrange(batch_major, p=P)
         gate_ps = {}
-        deterT = {}
+        updateT = {}
+        kept = {}
         reset = {}
         update = {}
         mix = {}
@@ -426,16 +489,22 @@ def tile_deter_pb_kernel(tc, hid0, deter, hw1, hb1, hg1, gw, gb, out):
                         stop=True,
                     )
 
-        def transpose_deter(unit):
-            deterT[unit] = psum_tile([P, TILES_PER_UNIT, BATCH], BF16, "inT")
+        def transpose_units(source, target):
             for s in range(TILES_PER_UNIT):
-                first = (unit * TILES_PER_UNIT + s) * P
                 for bt in range(BATCH_TILES):
                     nc.tensor.transpose(
-                        deterT[unit][:, s, bt * P : (bt + 1) * P],
-                        deter_sb[:, bt, first : first + P],
-                        ident_bf16[:],
+                        target[:, bt, s * P : (s + 1) * P],
+                        source[:, s, bt * P : (bt + 1) * P],
+                        ident_f32[:],
                     )
+
+        def transpose_update(unit):
+            updateT[unit] = psum_tile([P, BATCH_TILES, UNIT_COLS], F32, "inT")
+            transpose_units(update[unit], updateT[unit])
+
+        def transpose_mix(unit, tag):
+            mixT[unit] = psum_tile([P, BATCH_TILES, UNIT_COLS], F32, tag)
+            transpose_units(mix[unit], mixT[unit])
 
         def gate_bias(unit, gate, s):
             j, t = divmod(unit * TILES_PER_UNIT + s, FEAT_TILES)
@@ -468,38 +537,38 @@ def tile_deter_pb_kernel(tc, hid0, deter, hw1, hb1, hg1, gw, gb, out):
         def candidate(unit):
             nc.scalar.activation(out=mix[unit][:], in_=mix[unit][:], func=ACT.Tanh)
 
-        def mix_state(unit, multiplier):
-            nc.vector.tensor_tensor(
-                out=mix[unit][:], in0=mix[unit][:], in1=deterT[unit][:], op=ALU.subtract
-            )
+        def apply_update(unit, multiplier):
             multiplier.tensor_tensor(
                 out=mix[unit][:], in0=mix[unit][:], in1=update[unit][:], op=ALU.mult
             )
 
-        def transpose_mix(unit, tag):
-            mixT[unit] = psum_tile([P, BATCH_TILES, UNIT_COLS], F32, tag)
-            for s in range(TILES_PER_UNIT):
-                for bt in range(BATCH_TILES):
-                    nc.tensor.transpose(
-                        mixT[unit][:, bt, s * P : (s + 1) * P],
-                        mix[unit][:, s, bt * P : (bt + 1) * P],
-                        ident_f32[:],
-                    )
+        def unit_cols(unit):
+            return slice(unit * UNIT_COLS, (unit + 1) * UNIT_COLS)
+
+        def keep_state(unit):
+            kept[unit] = stage.tile([P, BATCH_TILES, UNIT_COLS], F32, name="kept", bufs=KEPT_BUFS)
+            nc.vector.scalar_tensor_tensor(
+                out=kept[unit][:],
+                in0=updateT[unit][:],
+                scalar=1.0,
+                in1=deter_sb[:, :, unit_cols(unit)],
+                op0=ALU.subtract,
+                op1=ALU.mult,
+            )
 
         def finish(unit):
-            cols = slice(unit * UNIT_COLS, (unit + 1) * UNIT_COLS)
             new_state = stage.tile([P, BATCH_TILES, UNIT_COLS], F32, bufs=STORE_BUFS)
             nc.vector.tensor_tensor(
-                out=new_state[:], in0=mixT[unit][:], in1=deter_sb[:, :, cols], op=ALU.add
+                out=new_state[:], in0=mixT[unit][:], in1=kept[unit][:], op=ALU.subtract
             )
-            nc.sync.dma_start(out=out_view[:, :, cols], in_=new_state[:])
+            nc.sync.dma_start(out=out_view[:, :, unit_cols(unit)], in_=new_state[:])
 
         gate_matmuls(0)
         for step in range(UNITS):
             sigmoids(step)
             if step + 1 < UNITS:
                 gate_matmuls(step + 1)
-            transpose_deter(step)
+            transpose_update(step)
             if step >= 1:
                 candidate(step - 1)
             reset_candidate(step)
@@ -508,9 +577,10 @@ def tile_deter_pb_kernel(tc, hid0, deter, hw1, hb1, hg1, gw, gb, out):
             if step >= 2:
                 transpose_mix(step - 2, "outT")
             if step == 0:
-                quantise_h(BLOCKS - 1)
                 for chunk in ready:
                     quantise_gw(chunk)
+            if step == H_STEP:
+                quantise_h(BLOCKS - 1)
             if G_CHUNKS and step >= 0:
                 piece = step - 1
                 chunk = CHUNKS - G_CHUNKS + piece // G_PIECES
@@ -521,13 +591,35 @@ def tile_deter_pb_kernel(tc, hid0, deter, hw1, hb1, hg1, gw, gb, out):
                 if piece > 0 and piece % G_PIECES == 0 and chunk <= CHUNKS:
                     quantise_gw(chunk - 1)
             if step >= 1:
-                mix_state(step - 1, nc.gpsimd)
+                keep_state(step - 1)
+                apply_update(step - 1, nc.gpsimd)
 
         last = UNITS - 1
-        candidate(last)
+        keep_state(last)
         finish(last - 2)
-        transpose_mix(last - 1, "outT")
-        mix_state(last, nc.vector)
-        transpose_mix(last, "inT")
+        for s in range(TILES_PER_UNIT):
+            nc.scalar.activation(out=mix[last][:, s, :], in_=mix[last][:, s, :], func=ACT.Tanh)
+        for s in range(TILES_PER_UNIT):
+            nc.vector.tensor_tensor(
+                out=mix[last][:, s, :], in0=mix[last][:, s, :], in1=update[last][:, s, :], op=ALU.mult
+            )
+        transpose_mix(last - 1, "mm")
+        halves = []
+        for s in range(TILES_PER_UNIT):
+            half = psum_tile([P, BATCH_TILES, P], F32, "mm")
+            for bt in range(BATCH_TILES):
+                nc.tensor.transpose(
+                    half[:, bt, :], mix[last][:, s, bt * P : (bt + 1) * P], ident_f32[:]
+                )
+            halves.append(half)
         finish(last - 1)
-        finish(last)
+        for s in range(TILES_PER_UNIT):
+            new_half = stage.tile([P, BATCH_TILES, P], F32, tag="f32_tile", bufs=F32_TILE_BUFS)
+            nc.vector.tensor_tensor(
+                out=new_half[:],
+                in0=halves[s][:],
+                in1=kept[last][:, :, s * P : (s + 1) * P],
+                op=ALU.subtract,
+            )
+            first = last * UNIT_COLS + s * P
+            nc.sync.dma_start(out=out_view[:, :, first : first + P], in_=new_half[:])

@@ -40,8 +40,8 @@ W1_LATE = [0, 0, 1, 0, 0, 0, 0, 0]
 W1_SPLITS = [384] * 4 + [512] * 4
 P1_SPLIT = 256
 P2_SPLIT = 224
-P1 = [0, 2, 1, 1, 1, 1, 0, 2]
-P1V = [0, 0, 0, 0, 0, 0, 1, 0]
+P1 = [0, 1, 1, 1, 1, 1, 1, 1]
+P1V = [0] * 8
 WAIT = 0
 WAIT2 = 1
 P2_ROUNDS = 7
@@ -51,7 +51,7 @@ H_STEP = 1
 GW_SPLIT = 1
 KEPT_BUFS = 3
 SEAM_SPLIT = 224
-SEAM_V = 1
+SEAM_V = 0
 PE_ROUNDS = 0
 BANK_COLS = 256
 TR_AHEAD = 2
@@ -68,12 +68,15 @@ GW_AHEAD = 3
 HID_AHEAD = 4
 W1_AHEAD = 2
 
-PSUM_BUFS = {"mm": 5, "inT": 2, "outT": 1}
+MATMUL_BANKS = (0, 1, 2, 3, 4)
+BANKS_IN_PASS_1 = 4
+TRANSPOSE_BANKS = (5, 6)
+OUT_BANK = 7
 STAGE_BUFS = 2
 GROUPED_BUFS = 4
 F32_TILE_BUFS = 2 * FEAT_TILES
 STEPS_ALIVE = 4
-STORE_BUFS = 3
+STORE_BUFS = 6
 
 FLOPS = 2 * BATCH * DPB * (DPB + GATES * DPB) * BLOCKS
 
@@ -96,8 +99,19 @@ def tile_deter_pb_kernel(tc, hid0, deter, hw1, hb1, hg1, gw, gb, out):
         psum = stack.enter_context(tc.psum_pool(name="psum", bufs=1))
         stack.enter_context(tc.manual_schedule())
 
+        turn = {"mm": 0, "inT": 0}
+
+        def bank_tile(shape, dtype, bank):
+            return psum.tile(shape, dtype, name="bank" + str(bank), tag="bank" + str(bank), bufs=1)
+
         def psum_tile(shape, dtype, tag):
-            return psum.tile(shape, dtype, name=tag + "_ps", tag=tag, bufs=PSUM_BUFS[tag])
+            banks = MATMUL_BANKS[: BANKS_IN_PASS_1 if first_pass[0] else len(MATMUL_BANKS)] if tag == "mm" else TRANSPOSE_BANKS
+            if tag == "outT":
+                return bank_tile(shape, dtype, OUT_BANK)
+            turn[tag] += 1
+            return bank_tile(shape, dtype, banks[turn[tag] % len(banks)])
+
+        first_pass = [True]
 
         batch_major = "(bt p) f -> p bt f"
 
@@ -105,8 +119,6 @@ def tile_deter_pb_kernel(tc, hid0, deter, hw1, hb1, hg1, gw, gb, out):
         make_identity(nc, ident_f32[:])
         ident_bf16 = const.tile([P, P], BF16)
         make_identity(nc, ident_bf16[:])
-        mean_weights = const.tile([P, P], F32)
-        nc.vector.memset(mean_weights[:], 1.0 / DETER)
         eps = const.tile([P, 1], F32)
         nc.vector.memset(eps[:], EPS)
         hidden_rows = const.tile([P, P], BF16)
@@ -118,8 +130,7 @@ def tile_deter_pb_kernel(tc, hid0, deter, hw1, hb1, hg1, gw, gb, out):
         hid_scales = keep.tile([P, BLOCKS, BATCH], U8, align_bytes=64)
         w1_codes = keep.tile([P, BLOCKS, DPB], U32, align_bytes=64)
         w1_scales = keep.tile([P, BLOCKS, DPB], U8, align_bytes=64)
-        h_codes = keep.tile([P, BLOCKS, BATCH], U32, align_bytes=64)
-        h_scales = keep.tile([P, BLOCKS, BATCH], U8, align_bytes=64)
+        h_codes, h_scales = hid_codes, hid_scales
         gw_codes = keep.tile([P, BLOCKS, GATES * DPB], U32, align_bytes=64)
         gw_scales = keep.tile([P, BLOCKS, GATES * DPB], U8, align_bytes=64)
 
@@ -336,7 +347,7 @@ def tile_deter_pb_kernel(tc, hid0, deter, hw1, hb1, hg1, gw, gb, out):
             out=gb_cols[:].rearrange("p j g t -> p (j g t)"), in_=gate_cols_ps[:, 0 : GATES * N_TILES]
         )
 
-        mean_ps = psum_tile([P, BATCH], F32, "outT")
+        sums_ps = [bank_tile([P, P], F32, bank) for bank in (MATMUL_BANKS[-1], OUT_BANK)]
         done = 0
         ready = []
         for j in range(BLOCKS):
@@ -353,13 +364,15 @@ def tile_deter_pb_kernel(tc, hid0, deter, hw1, hb1, hg1, gw, gb, out):
                 nc.scalar.activation(
                     out=squares[:], in_=u_tile(m), func=ACT.Square, bias=hb_cols[:, m : m + 1]
                 )
-                nc.tensor.matmul(
-                    out=mean_ps[:],
-                    lhsT=mean_weights[:],
-                    rhs=squares[:],
-                    start=(m == 0),
-                    stop=(m == N_TILES - 1),
-                )
+                for bt in range(BATCH_TILES):
+                    nc.tensor.matmul(
+                        out=sums_ps[bt][:],
+                        lhsT=squares[:, bt * P : (bt + 1) * P],
+                        rhs=ident_f32[:],
+                        is_transpose=True,
+                        start=(m == 0),
+                        stop=(m == N_TILES - 1),
+                    )
             if j + 2 < BLOCKS and not W1_LATE[j]:
                 regroup_w1(j + 2)
             if j + TR_AHEAD == BLOCKS - 1:
@@ -387,22 +400,37 @@ def tile_deter_pb_kernel(tc, hid0, deter, hw1, hb1, hg1, gw, gb, out):
             out=gb_cols[:, :, UPDATE, :], in0=gb_cols[:, :, UPDATE, :], scalar1=-1.0
         )
         table(ACT.Sqrt)
+        first_pass[0] = False
+        total = const.tile([P, BATCH_TILES], F32)
+        for bt in range(BATCH_TILES):
+            nc.vector.tensor_reduce(
+                out=total[:, bt : bt + 1], in_=sums_ps[bt][:], op=ALU.add, axis=mybir.AxisListType.X
+            )
+        rms = const.tile([P, BATCH_TILES], F32)
+        nc.scalar.activation(
+            out=rms[:], in_=total[:], func=ACT.Sqrt, scale=1.0 / DETER, bias=eps[:, 0:1]
+        )
+        share(done, SEAM_SPLIT)
+        later = [done]
+        done += 1
+        table(ACT.Silu)
+        rstd_col = const.tile([P, BATCH_TILES], F32)
+        nc.vector.reciprocal(out=rstd_col[:], in_=rms[:])
+        rstd_ps = psum_tile([P, BATCH_TILES, P], F32, "inT")
+        for bt in range(BATCH_TILES):
+            nc.tensor.transpose(
+                rstd_ps[:, bt, :], rstd_col[:, bt : bt + 1].to_broadcast([P, P]), ident_f32[:]
+            )
+        hidden_matmuls(0)
         for chunk in ready:
             quantise_gw(chunk)
-        ready = []
-        hidden_matmuls(0)
+        ready = later
         for n in range(SEAM_V):
             share(done, DPB)
             ready.append(done)
             done += 1
-        rms = const.tile([P, BATCH], F32)
-        nc.scalar.activation(out=rms[:], in_=mean_ps[:], func=ACT.Sqrt, bias=eps[:, 0:1])
-        share(done, SEAM_SPLIT)
-        ready.append(done)
-        done += 1
-        table(ACT.Silu)
         rstd = const.tile([P, BATCH], F32)
-        nc.vector.reciprocal(out=rstd[:], in_=rms[:])
+        nc.vector.tensor_copy(out=rstd[:], in_=rstd_ps[:].rearrange("p t b -> p (t b)"))
 
         rest = CHUNKS - done - G_CHUNKS - LASTV - PE_ROUNDS
         h_grouped = {}

@@ -39,7 +39,7 @@ W1_BUFS = 4
 W1_LATE = [0, 0, 1, 0, 0, 0, 0, 0]
 W1_SPLITS = [384] * 4 + [512] * 4
 P1_SPLIT = 256
-P2_SPLIT = 224
+P2_SPLIT = 256
 P1 = [0, 1, 1, 1, 1, 1, 1, 1]
 P1V = [0] * 8
 WAIT = 0
@@ -52,7 +52,7 @@ GW_SPLIT = 1
 KEPT_BUFS = 3
 SEAM_SPLIT = 224
 SEAM_V = 0
-PE_ROUNDS = 0
+PE_ROUNDS = 6
 BANK_COLS = 256
 TR_AHEAD = 2
 COPY_FIRST = True
@@ -274,11 +274,12 @@ def tile_deter_pb_kernel(tc, hid0, deter, hw1, hb1, hg1, gw, gb, out):
             banks = []
             for lo in range(0, DPB, BANK_COLS):
                 bank = psum_tile([P, BANK_COLS, PACK], BF16, "inT")
-                for t in range(PACK):
+                for c in range(0, BANK_COLS, P):
+                    first = gate * DPB + lo + c
                     nc.tensor.matmul(
-                        out=bank[:, :, t],
+                        out=bank[:, c : c + P, :].rearrange("p n t -> p (n t)"),
                         lhsT=ident_bf16[:],
-                        rhs=gw_rows[block][:, t, gate * DPB + lo : gate * DPB + lo + BANK_COLS],
+                        rhs=gw_rows[block][:, :, first : first + P].rearrange("p t n -> p n t"),
                         start=True,
                         stop=True,
                     )

@@ -40,20 +40,21 @@ W1_LATE = [0, 0, 1, 0, 0, 0, 0, 0]
 W1_SPLITS = [384] * 4 + [512] * 4
 P1_SPLIT = 256
 P2_SPLIT = 256
-P1 = [0, 1, 1, 1, 1, 1, 1, 1]
+P1 = [0, 1, 1, 1, 1, 1, 1, 2]
 P1V = [0] * 8
 WAIT = 0
 WAIT2 = 1
 P2_ROUNDS = 7
 G_CHUNKS = 0
 LASTV = 1
+HID_SPLIT = 1
+W1_HALVES = 0
 H_STEP = 1
 GW_SPLIT = 1
 KEPT_BUFS = 3
 SEAM_SPLIT = 224
 SEAM_V = 0
-PE_ROUNDS = 6
-BANK_COLS = 256
+PE_HALVES = [1, 2, 1, 2, 1, 2, 1, 2]
 TR_AHEAD = 2
 COPY_FIRST = True
 HID_EARLY = False
@@ -139,17 +140,29 @@ def tile_deter_pb_kernel(tc, hid0, deter, hw1, hb1, hg1, gw, gb, out):
         gw_rows = {}
 
         def load_hid0(pair):
-            cols = slice(pair * PAIR * DPB, (pair + 1) * PAIR * DPB)
-            nc.sync.dma_start(
-                out=hid_sb[:, pair, :, :], in_=hid0.rearrange(batch_major, p=P)[:, :, cols]
-            )
+            parts = PAIR if pair < HID_SPLIT else 1
+            width = PAIR * DPB // parts
+            for part in range(parts):
+                first = pair * PAIR * DPB + part * width
+                nc.sync.dma_start(
+                    out=hid_sb[:, pair, :, part * width : (part + 1) * width],
+                    in_=hid0.rearrange(batch_major, p=P)[:, :, first : first + width],
+                )
 
         def load_w1(j):
             w1_rows[j] = wraw.tile([P, PACK, DPB], BF16, name="w1_rows", bufs=W1_BUFS)
-            nc.sync.dma_start(
-                out=w1_rows[j][:].rearrange("p (u e) n -> p u (e n)", e=2),
-                in_=hw1[j].rearrange("(u p e) n -> p u (e n)", u=WORDS, e=2),
-            )
+            if j < W1_HALVES:
+                for lo in range(0, DPB, DPB // 2):
+                    cols = slice(lo, lo + DPB // 2)
+                    nc.sync.dma_start(
+                        out=w1_rows[j][:, :, cols].rearrange("p (u e) n -> p u e n", e=2),
+                        in_=hw1[j].rearrange("(u p e) n -> p u e n", u=WORDS, e=2)[:, :, :, cols],
+                    )
+            else:
+                nc.sync.dma_start(
+                    out=w1_rows[j][:].rearrange("p (u e) n -> p u (e n)", e=2),
+                    in_=hw1[j].rearrange("(u p e) n -> p u (e n)", u=WORDS, e=2),
+                )
 
         def load_gw(block):
             gw_rows[block] = wraw.tile(
@@ -225,7 +238,9 @@ def tile_deter_pb_kernel(tc, hid0, deter, hw1, hb1, hg1, gw, gb, out):
         def regroup_w1(j):
             w1_grouped[j] = grouped_tile()
             split = W1_SPLITS[j]
-            for copy, lo, hi in ((nc.vector.tensor_copy, 0, split), (nc.scalar.copy, split, DPB)):
+            vector_ends = [0, DPB // 2, split] if j < W1_HALVES and split > DPB // 2 else [0, split]
+            shares = [(nc.vector.tensor_copy, lo, hi) for lo, hi in zip(vector_ends, vector_ends[1:])]
+            for copy, lo, hi in shares + [(nc.scalar.copy, split, DPB)]:
                 if lo < hi:
                     regroup(copy, w1_grouped[j][:, lo:hi, :], w1_rows[j][:, :, lo:hi])
             if j + W1_BUFS < BLOCKS:
@@ -268,28 +283,19 @@ def tile_deter_pb_kernel(tc, hid0, deter, hw1, hb1, hg1, gw, gb, out):
                 in_=gw_grouped[chunk][:].rearrange("p w t -> p (w t)"),
             )
 
-        def tensor_regroup(chunk):
+        def tensor_regroup(chunk, lo):
             block, gate = divmod(chunk, GATES)
-            gw_grouped[chunk] = grouped_tile()
-            banks = []
-            for lo in range(0, DPB, BANK_COLS):
-                bank = psum_tile([P, BANK_COLS, PACK], BF16, "inT")
-                for c in range(0, BANK_COLS, P):
-                    first = gate * DPB + lo + c
-                    nc.tensor.matmul(
-                        out=bank[:, c : c + P, :].rearrange("p n t -> p (n t)"),
-                        lhsT=ident_bf16[:],
-                        rhs=gw_rows[block][:, :, first : first + P].rearrange("p t n -> p n t"),
-                        start=True,
-                        stop=True,
-                    )
-                banks.append((lo, bank))
-            free_gw(chunk)
-            return banks
-
-        def copy_banks(chunk, banks):
-            for lo, bank in banks:
-                nc.scalar.copy(out=gw_grouped[chunk][:, lo : lo + BANK_COLS, :], in_=bank[:])
+            bank = psum_tile([P, PIECE, PACK], BF16, "inT")
+            for c in range(0, PIECE, P):
+                first = gate * DPB + lo + c
+                nc.tensor.matmul(
+                    out=bank[:, c : c + P, :].rearrange("p n t -> p (n t)"),
+                    lhsT=ident_bf16[:],
+                    rhs=gw_rows[block][:, :, first : first + P].rearrange("p t n -> p n t"),
+                    start=True,
+                    stop=True,
+                )
+            return bank
 
         def share(chunk, split):
             regroup_gw(nc.vector.tensor_copy, chunk, 0, split)
@@ -400,7 +406,6 @@ def tile_deter_pb_kernel(tc, hid0, deter, hw1, hb1, hg1, gw, gb, out):
         nc.vector.tensor_scalar_add(
             out=gb_cols[:, :, UPDATE, :], in0=gb_cols[:, :, UPDATE, :], scalar1=-1.0
         )
-        table(ACT.Sqrt)
         first_pass[0] = False
         total = const.tile([P, BATCH_TILES], F32)
         for bt in range(BATCH_TILES):
@@ -433,7 +438,9 @@ def tile_deter_pb_kernel(tc, hid0, deter, hw1, hb1, hg1, gw, gb, out):
         rstd = const.tile([P, BATCH], F32)
         nc.vector.tensor_copy(out=rstd[:], in_=rstd_ps[:].rearrange("p t b -> p (t b)"))
 
-        rest = CHUNKS - done - G_CHUNKS - LASTV - PE_ROUNDS
+        rest = CHUNKS - done - G_CHUNKS - LASTV - sum(PE_HALVES) // 2
+        tensor_half = 0
+        tensor_chunk = 0
         h_grouped = {}
 
         def quantise_h(j):
@@ -447,10 +454,15 @@ def tile_deter_pb_kernel(tc, hid0, deter, hw1, hb1, hg1, gw, gb, out):
             if j + 1 < BLOCKS:
                 hidden_matmuls(j + 1)
             banks = []
-            by_tensor = done
-            if j < PE_ROUNDS:
-                done += 1
-                banks = tensor_regroup(by_tensor)
+            for n in range(PE_HALVES[j]):
+                if tensor_half == 0:
+                    tensor_chunk = done
+                    done += 1
+                    gw_grouped[tensor_chunk] = grouped_tile()
+                banks.append((tensor_chunk, tensor_half, tensor_regroup(tensor_chunk, tensor_half * PIECE)))
+                if tensor_half == 1:
+                    free_gw(tensor_chunk)
+                tensor_half = 1 - tensor_half
             h_rows = stage.tile([P, PACK, BATCH], BF16)
             for t in range(FEAT_TILES):
                 m = j * FEAT_TILES + t
@@ -469,9 +481,12 @@ def tile_deter_pb_kernel(tc, hid0, deter, hw1, hb1, hg1, gw, gb, out):
             for chunk in ready:
                 quantise_gw(chunk)
             ready = []
-            if banks:
-                copy_banks(by_tensor, banks)
-                ready.append(by_tensor)
+            for chunk, half, bank in banks:
+                nc.scalar.copy(
+                    out=gw_grouped[chunk][:, half * PIECE : (half + 1) * PIECE, :], in_=bank[:]
+                )
+                if half == 1:
+                    ready.append(chunk)
             count = (j + 1) * rest // P2_ROUNDS - j * rest // P2_ROUNDS if j < P2_ROUNDS else 0
             if j >= 1 and count == 0:
                 quantise_h(j - 1)

@@ -38,8 +38,8 @@ FIRST_LATE_CHUNK = EARLY_CHUNKS + WAIT_CHUNKS
 W1_BUFS = 4
 W1_LATE = [0, 0, 1, 0, 0, 0, 0, 0]
 W1_SPLITS = [384] * 4 + [512] * 4
-P1_SPLIT = 256
-P2_SPLIT = 256
+P1_SPLIT = 288
+P2_SPLIT = 288
 P1 = [0, 1, 1, 1, 1, 1, 1, 2]
 P1V = [0] * 8
 WAIT = 0
@@ -47,6 +47,7 @@ WAIT2 = 1
 P2_ROUNDS = 7
 G_CHUNKS = 0
 LASTV = 1
+G_ROWS = 192
 HID_SPLIT = 1
 W1_HALVES = 0
 H_STEP = 1
@@ -441,6 +442,7 @@ def tile_deter_pb_kernel(tc, hid0, deter, hw1, hb1, hg1, gw, gb, out):
         rest = CHUNKS - done - G_CHUNKS - LASTV - sum(PE_HALVES) // 2
         tensor_half = 0
         tensor_chunk = 0
+        h_rows_of = {}
         h_grouped = {}
 
         def quantise_h(j):
@@ -478,6 +480,8 @@ def tile_deter_pb_kernel(tc, hid0, deter, hw1, hb1, hg1, gw, gb, out):
                 nc.scalar.activation(
                     out=h_rows[:, t, :], in_=normed[:], func=ACT.Silu, scale=hg_cols[:, m : m + 1]
                 )
+            if j >= 1 and G_ROWS < BATCH:
+                regroup(nc.vector.tensor_copy, h_grouped[j - 1][:, G_ROWS:, :], h_rows_of[j - 1][:, :, G_ROWS:])
             for chunk in ready:
                 quantise_gw(chunk)
             ready = []
@@ -502,7 +506,8 @@ def tile_deter_pb_kernel(tc, hid0, deter, hw1, hb1, hg1, gw, gb, out):
                     ready.append(done)
                     done += 1
             h_grouped[j] = stage.tile([P, BATCH, PACK], BF16, name="h_grouped", bufs=1, align_bytes=64)
-            regroup(gpsimd_copy, h_grouped[j][:], h_rows[:])
+            h_rows_of[j] = h_rows
+            regroup(gpsimd_copy, h_grouped[j][:, 0:G_ROWS, :], h_rows[:, :, 0:G_ROWS])
         table(ACT.Sigmoid)
 
         out_view = out.rearrange(batch_major, p=P)
@@ -623,6 +628,8 @@ def tile_deter_pb_kernel(tc, hid0, deter, hw1, hb1, hg1, gw, gb, out):
             if step == 0:
                 for chunk in ready:
                     quantise_gw(chunk)
+            if step == 0 and G_ROWS < BATCH:
+                regroup(nc.vector.tensor_copy, h_grouped[BLOCKS - 1][:, G_ROWS:, :], h_rows_of[BLOCKS - 1][:, :, G_ROWS:])
             if step == H_STEP:
                 quantise_h(BLOCKS - 1)
             if G_CHUNKS and step >= 0:

from contextlib import ExitStack

import concourse.mybir as mybir
from concourse.masks import make_identity

F32 = mybir.dt.float32
BF16 = mybir.dt.bfloat16
U32 = mybir.dt.uint32
U8 = mybir.dt.uint8
FP8X4 = mybir.dt.float8_e4m3fn_x4
ACT = mybir.ActivationFunctionType
ALU = mybir.AluOpType

P = 128
PACK = 4
WORDS = PACK // 2
BATCH = 256
BATCH_TILES = BATCH // P
DETER = 4096
BLOCKS = 8
DPB = DETER // BLOCKS
FEAT_TILES = DPB // P
N_TILES = DETER // P
GATES = 3
RESET, CAND, UPDATE = 0, 1, 2
EPS = 1e-4

TILES_PER_UNIT = 2
UNITS_PER_BLOCK = FEAT_TILES // TILES_PER_UNIT
UNITS = BLOCKS * UNITS_PER_BLOCK
UNIT_COLS = TILES_PER_UNIT * P

CHUNKS = BLOCKS * GATES
PIECE = DPB // 2
EARLY_CHUNKS = 2 * (BLOCKS - 2)
WAIT_CHUNKS = 2
FIRST_LATE_CHUNK = EARLY_CHUNKS + WAIT_CHUNKS
W1_BUFS = 4
W1_LATE = [0, 0, 1, 0, 0, 0, 0, 0]
W1_SPLITS = [384] * 4 + [512] * 4
P1_SPLIT = 288
P2_SPLIT = 288
P1 = [0, 1, 1, 1, 1, 1, 1, 2]
P1V = [0] * 8
WAIT = 0
WAIT2 = 1
P2_ROUNDS = 7
G_CHUNKS = 0
LASTV = 1
G_ROWS = 192
HID_SPLIT = 1
W1_HALVES = 0
H_STEP = 1
GW_SPLIT = 1
KEPT_BUFS = 3
SEAM_SPLIT = 224
SEAM_V = 0
PE_HALVES = [1, 2, 1, 2, 1, 2, 1, 2]
TR_AHEAD = 2
COPY_FIRST = True
HID_EARLY = False
SEAM_Q = 3
G_PIECES = 2
LOADS_AFTER_W1 = {2: [('h', 3), ('g', 1)], 3: [('g', 2)]}

PAIR = 2
PAIRS = BLOCKS // PAIR
W1_PAIRS_AHEAD = 2
GW_AHEAD = 3
HID_AHEAD = 4
W1_AHEAD = 2

MATMUL_BANKS = (0, 1, 2, 3, 4)
BANKS_IN_PASS_1 = 4
TRANSPOSE_BANKS = (5, 6)
OUT_BANK = 7
STAGE_BUFS = 2
GROUPED_BUFS = 4
F32_TILE_BUFS = 2 * FEAT_TILES
STEPS_ALIVE = 4
STORE_BUFS = 6

FLOPS = 2 * BATCH * DPB * (DPB + GATES * DPB) * BLOCKS


def regroup(copy, grouped, rows):
    copy(
        out=grouped.rearrange("p (c i) t -> p c t i", i=4),
        in_=rows.rearrange("p t (c i) -> p c t i", i=4),
    )


def tile_deter_pb_kernel(tc, hid0, deter, hw1, hb1, hg1, gw, gb, out):
    nc = tc.nc
    with ExitStack() as stack:
        const = stack.enter_context(tc.tile_pool(name="const", bufs=1))
        acts = stack.enter_context(tc.tile_pool(name="acts", bufs=1))
        wraw = stack.enter_context(tc.tile_pool(name="wraw", bufs=1))
        keep = stack.enter_context(tc.tile_pool(name="keep", bufs=1))
        stage = stack.enter_context(tc.tile_pool(name="stage", bufs=STAGE_BUFS))
        psum = stack.enter_context(tc.psum_pool(name="psum", bufs=1))
        stack.enter_context(tc.manual_schedule())

        turn = {"mm": 0, "inT": 0}

        def bank_tile(shape, dtype, bank):
            return psum.tile(shape, dtype, name="bank" + str(bank), tag="bank" + str(bank), bufs=1)

        def psum_tile(shape, dtype, tag):
            banks = MATMUL_BANKS[: BANKS_IN_PASS_1 if first_pass[0] else len(MATMUL_BANKS)] if tag == "mm" else TRANSPOSE_BANKS
            if tag == "outT":
                return bank_tile(shape, dtype, OUT_BANK)
            turn[tag] += 1
            return bank_tile(shape, dtype, banks[turn[tag] % len(banks)])

        first_pass = [True]

        batch_major = "(bt p) f -> p bt f"

        ident_f32 = const.tile([P, P], F32)
        make_identity(nc, ident_f32[:])
        ident_bf16 = const.tile([P, P], BF16)
        make_identity(nc, ident_bf16[:])
        eps = const.tile([P, 1], F32)
        nc.vector.memset(eps[:], EPS)
        hidden_rows = const.tile([P, P], BF16)
        nc.vector.memset(hidden_rows[:], 0.0)
        gate_rows = const.tile([P, P], BF16)
        nc.vector.memset(gate_rows[:], 0.0)

        hid_codes = keep.tile([P, BLOCKS, BATCH], U32, align_bytes=64)
        hid_scales = keep.tile([P, BLOCKS, BATCH], U8, align_bytes=64)
        w1_codes = keep.tile([P, BLOCKS, DPB], U32, align_bytes=64)
        w1_scales = keep.tile([P, BLOCKS, DPB], U8, align_bytes=64)
        h_codes, h_scales = hid_codes, hid_scales
        gw_codes = keep.tile([P, BLOCKS, GATES * DPB], U32, align_bytes=64)
        gw_scales = keep.tile([P, BLOCKS, GATES * DPB], U8, align_bytes=64)

        hid_sb = acts.tile([P, PAIRS, BATCH_TILES, PAIR * DPB], BF16, tag="acts")
        w1_rows = {}
        gw_rows = {}

        def load_hid0(pair):
            parts = PAIR if pair < HID_SPLIT else 1
            width = PAIR * DPB // parts
            for part in range(parts):
                first = pair * PAIR * DPB + part * width
                nc.sync.dma_start(
                    out=hid_sb[:, pair, :, part * width : (part + 1) * width],
                    in_=hid0.rearrange(batch_major, p=P)[:, :, first : first + width],
                )

        def load_w1(j):
            w1_rows[j] = wraw.tile([P, PACK, DPB], BF16, name="w1_rows", bufs=W1_BUFS)
            if j < W1_HALVES:
                for lo in range(0, DPB, DPB // 2):
                    cols = slice(lo, lo + DPB // 2)
                    nc.sync.dma_start(
                        out=w1_rows[j][:, :, cols].rearrange("p (u e) n -> p u e n", e=2),
                        in_=hw1[j].rearrange("(u p e) n -> p u e n", u=WORDS, e=2)[:, :, :, cols],
                    )
            else:
                nc.sync.dma_start(
                    out=w1_rows[j][:].rearrange("p (u e) n -> p u (e n)", e=2),
                    in_=hw1[j].rearrange("(u p e) n -> p u (e n)", u=WORDS, e=2),
                )

        def load_gw(block):
            gw_rows[block] = wraw.tile(
                [P, PACK, GATES * DPB], BF16, name="gw_rows", bufs=GW_AHEAD
            )
            parts = GATES if block < GW_SPLIT else 1
            width = GATES * DPB // parts
            for part in range(parts):
                cols = slice(part * width, (part + 1) * width)
                nc.sync.dma_start(
                    out=gw_rows[block][:, :, cols],
                    in_=gw[block].rearrange("(t p) n -> p t n", p=P)[:, :, cols],
                )

        nc.scalar.dma_start(out=hidden_rows[0:N_TILES, :], in_=hb1.rearrange("(m p) -> m p", p=P))
        nc.scalar.dma_start(
            out=hidden_rows[N_TILES : 2 * N_TILES, :], in_=hg1.rearrange("(m p) -> m p", p=P)
        )
        nc.scalar.dma_start(
            out=gate_rows[0 : GATES * N_TILES, :], in_=gb.rearrange("(m p) -> m p", p=P)
        )
        load_w1(0)
        load_hid0(0)
        load_w1(1)
        load_hid0(1)
        load_w1(2)
        load_w1(3)
        if HID_EARLY:
            load_hid0(2)
        load_gw(0)
        if not HID_EARLY:
            load_hid0(2)

        hid_words = hid_sb[:].bitcast(F32)
        words_per_block = DPB // 2
        hidT = {}

        def transpose_hid0(j):
            pair, i = divmod(j, PAIR)
            hidT[j] = psum_tile([P, WORDS, BATCH], F32, "inT")
            for u in range(WORDS):
                first = i * words_per_block + u * P
                for bt in range(BATCH_TILES):
                    nc.tensor.transpose(
                        hidT[j][:, u, bt * P : (bt + 1) * P],
                        hid_words[:, pair, bt, first : first + P],
                        ident_f32[:],
                    )

        hid_grouped = {}

        def copy_hid0(j):
            hid_grouped[j] = stage.tile([P, BATCH * PACK], BF16, name="hid_grouped", align_bytes=64)
            nc.scalar.copy(
                out=hid_grouped[j][:].bitcast(F32).rearrange("p (b u) -> p b u", u=WORDS),
                in_=hidT[j][:].rearrange("p u b -> p b u"),
            )

        def quantise_hid0(j):
            nc.vector.quantize_mx(
                out=hid_codes[:, j, :].bitcast(FP8X4),
                scales=hid_scales[:, j, :],
                in_=hid_grouped[j][:],
            )

        def grouped_tile():
            return stage.tile(
                [P, DPB, PACK], BF16, name="grouped", bufs=GROUPED_BUFS, align_bytes=64
            )

        w1_grouped = {}

        def regroup_w1(j):
            w1_grouped[j] = grouped_tile()
            split = W1_SPLITS[j]
            vector_ends = [0, DPB // 2, split] if j < W1_HALVES and split > DPB // 2 else [0, split]
            shares = [(nc.vector.tensor_copy, lo, hi) for lo, hi in zip(vector_ends, vector_ends[1:])]
            for copy, lo, hi in shares + [(nc.scalar.copy, split, DPB)]:
                if lo < hi:
                    regroup(copy, w1_grouped[j][:, lo:hi, :], w1_rows[j][:, :, lo:hi])
            if j + W1_BUFS < BLOCKS:
                load_w1(j + W1_BUFS)
            if j in LOADS_AFTER_W1:
                for kind, n in LOADS_AFTER_W1[j]:
                    (load_hid0 if kind == "h" else load_gw)(n)

        def quantise_w1(j):
            nc.vector.quantize_mx(
                out=w1_codes[:, j, :].bitcast(FP8X4),
                scales=w1_scales[:, j, :],
                in_=w1_grouped[j][:].rearrange("p w t -> p (w t)"),
            )

        gw_grouped = {}

        def regroup_gw(copy, chunk, lo, hi):
            block, gate = divmod(chunk, GATES)
            if chunk not in gw_grouped:
                gw_grouped[chunk] = grouped_tile()
            if lo < hi:
                regroup(
                    copy,
                    gw_grouped[chunk][:, lo:hi, :],
                    gw_rows[block][:, :, gate * DPB + lo : gate * DPB + hi],
                )

        def free_gw(chunk):
            block, gate = divmod(chunk, GATES)
            if gate == GATES - 1 and block + GW_AHEAD < BLOCKS:
                load_gw(block + GW_AHEAD)

        def quantise_gw(chunk):
            block, gate = divmod(chunk, GATES)
            cols = slice(gate * DPB, (gate + 1) * DPB)
            nc.vector.quantize_mx(
                out=gw_codes[:, block, cols].bitcast(FP8X4),
                scales=gw_scales[:, block, cols],
                in_=gw_grouped[chunk][:].rearrange("p w t -> p (w t)"),
            )

        def tensor_regroup(chunk, lo):
            block, gate = divmod(chunk, GATES)
            bank = psum_tile([P, PIECE, PACK], BF16, "inT")
            for c in range(0, PIECE, P):
                first = gate * DPB + lo + c
                nc.tensor.matmul(
                    out=bank[:, c : c + P, :].rearrange("p n t -> p (n t)"),
                    lhsT=ident_bf16[:],
                    rhs=gw_rows[block][:, :, first : first + P].rearrange("p t n -> p n t"),
                    start=True,
                    stop=True,
                )
            return bank

        def share(chunk, split):
            regroup_gw(nc.vector.tensor_copy, chunk, 0, split)
            regroup_gw(nc.scalar.copy, chunk, split, DPB)
            free_gw(chunk)

        def gpsimd_copy(out, in_):
            nc.gpsimd.tensor_scalar(
                out=out, in0=in_, scalar1=1.0, scalar2=0.0, op0=ALU.mult, op1=ALU.add
            )

        u_ps = {}

        def hidden_matmuls(j):
            for unit in range(j * UNITS_PER_BLOCK, (j + 1) * UNITS_PER_BLOCK):
                u_ps[unit] = psum_tile([P, TILES_PER_UNIT, BATCH], F32, "mm")
                for s in range(TILES_PER_UNIT):
                    first = (unit * TILES_PER_UNIT + s) * P - j * DPB
                    nc.tensor.matmul_mx(
                        out=u_ps[unit][:, s, :],
                        lhsT=w1_codes[:, j, first : first + P].bitcast(FP8X4),
                        lhsT_scale=w1_scales[:, j, first : first + P],
                        rhs=hid_codes[:, j, :].bitcast(FP8X4),
                        rhs_scale=hid_scales[:, j, :],
                        start=True,
                        stop=True,
                    )

        def u_tile(m):
            return u_ps[m // TILES_PER_UNIT][:, m % TILES_PER_UNIT, :]

        def table(func):
            nc.scalar.activation(out=scrap[:], in_=eps[:], func=func)

        scrap = const.tile([P, 1], F32)
        table(ACT.Sqrt)
        regroup_w1(0)
        transpose_hid0(0)
        transpose_hid0(1)
        copy_hid0(0)
        quantise_w1(0)
        copy_hid0(1)
        hidden_cols_ps = psum_tile([P, P], BF16, "mm")
        nc.tensor.transpose(hidden_cols_ps[:], hidden_rows[:], ident_bf16[:])
        hidden_cols = const.tile([P, 2 * N_TILES], F32)
        gate_cols_ps = psum_tile([P, P], BF16, "mm")
        nc.tensor.transpose(gate_cols_ps[:], gate_rows[:], ident_bf16[:])
        quantise_hid0(0)
        nc.vector.tensor_copy(out=hidden_cols[:], in_=hidden_cols_ps[:, 0 : 2 * N_TILES])
        hb_cols = hidden_cols[:, 0:N_TILES]
        hg_cols = hidden_cols[:, N_TILES : 2 * N_TILES]
        gb_cols = const.tile([P, BLOCKS, GATES, FEAT_TILES], F32)
        hidden_matmuls(0)
        regroup_w1(1)
        nc.vector.tensor_copy(
            out=gb_cols[:].rearrange("p j g t -> p (j g t)"), in_=gate_cols_ps[:, 0 : GATES * N_TILES]
        )

        sums_ps = [bank_tile([P, P], F32, bank) for bank in (MATMUL_BANKS[-1], OUT_BANK)]
        done = 0
        ready = []
        for j in range(BLOCKS):
            if j == 0 and TR_AHEAD == 3:
                transpose_hid0(2)
            if j + TR_AHEAD < BLOCKS:
                transpose_hid0(j + TR_AHEAD)
            if j + 1 < BLOCKS:
                quantise_hid0(j + 1)
                quantise_w1(j + 1)
                hidden_matmuls(j + 1)
            for m in range(j * FEAT_TILES, (j + 1) * FEAT_TILES):
                squares = stage.tile([P, BATCH], F32, tag="f32_tile", bufs=F32_TILE_BUFS)
                nc.scalar.activation(
                    out=squares[:], in_=u_tile(m), func=ACT.Square, bias=hb_cols[:, m : m + 1]
                )
                for bt in range(BATCH_TILES):
                    nc.tensor.matmul(
                        out=sums_ps[bt][:],
                        lhsT=squares[:, bt * P : (bt + 1) * P],
                        rhs=ident_f32[:],
                        is_transpose=True,
                        start=(m == 0),
                        stop=(m == N_TILES - 1),
                    )
            if j + 2 < BLOCKS and not W1_LATE[j]:
                regroup_w1(j + 2)
            if j + TR_AHEAD == BLOCKS - 1:
                deter_sb = acts.tile([P, BATCH_TILES, DETER], BF16, tag="acts")
            for chunk in ready:
                quantise_gw(chunk)
            ready = []
            if j + 2 < BLOCKS and COPY_FIRST:
                copy_hid0(j + 2)
            for n in range(P1[j]):
                share(done, P1_SPLIT)
                ready.append(done)
                done += 1
            for n in range(P1V[j]):
                share(done, DPB)
                ready.append(done)
                done += 1
            if j + 2 < BLOCKS and W1_LATE[j]:
                regroup_w1(j + 2)
            if j + 2 < BLOCKS and not COPY_FIRST:
                copy_hid0(j + 2)
        if True:
            nc.sync.dma_start(out=deter_sb[:], in_=deter.rearrange(batch_major, p=P))
        nc.vector.tensor_scalar_add(
            out=gb_cols[:, :, UPDATE, :], in0=gb_cols[:, :, UPDATE, :], scalar1=-1.0
        )
        first_pass[0] = False
        total = const.tile([P, BATCH_TILES], F32)
        for bt in range(BATCH_TILES):
            nc.vector.tensor_reduce(
                out=total[:, bt : bt + 1], in_=sums_ps[bt][:], op=ALU.add, axis=mybir.AxisListType.X
            )
        rms = const.tile([P, BATCH_TILES], F32)
        nc.scalar.activation(
            out=rms[:], in_=total[:], func=ACT.Sqrt, scale=1.0 / DETER, bias=eps[:, 0:1]
        )
        share(done, SEAM_SPLIT)
        later = [done]
        done += 1
        table(ACT.Silu)
        rstd_col = const.tile([P, BATCH_TILES], F32)
        nc.vector.reciprocal(out=rstd_col[:], in_=rms[:])
        rstd_ps = psum_tile([P, BATCH_TILES, P], F32, "inT")
        for bt in range(BATCH_TILES):
            nc.tensor.transpose(
                rstd_ps[:, bt, :], rstd_col[:, bt : bt + 1].to_broadcast([P, P]), ident_f32[:]
            )
        hidden_matmuls(0)
        for chunk in ready:
            quantise_gw(chunk)
        ready = later
        for n in range(SEAM_V):
            share(done, DPB)
            ready.append(done)
            done += 1
        rstd = const.tile([P, BATCH], F32)
        nc.vector.tensor_copy(out=rstd[:], in_=rstd_ps[:].rearrange("p t b -> p (t b)"))

        rest = CHUNKS - done - G_CHUNKS - LASTV - sum(PE_HALVES) // 2
        tensor_half = 0
        tensor_chunk = 0
        h_rows_of = {}
        h_grouped = {}

        def quantise_h(j):
            nc.vector.quantize_mx(
                out=h_codes[:, j, :].bitcast(FP8X4),
                scales=h_scales[:, j, :],
                in_=h_grouped[j][:].rearrange("p w t -> p (w t)"),
            )

        for j in range(BLOCKS):
            if j + 1 < BLOCKS:
                hidden_matmuls(j + 1)
            banks = []
            for n in range(PE_HALVES[j]):
                if tensor_half == 0:
                    tensor_chunk = done
                    done += 1
                    gw_grouped[tensor_chunk] = grouped_tile()
                banks.append((tensor_chunk, tensor_half, tensor_regroup(tensor_chunk, tensor_half * PIECE)))
                if tensor_half == 1:
                    free_gw(tensor_chunk)
                tensor_half = 1 - tensor_half
            h_rows = stage.tile([P, PACK, BATCH], BF16)
            for t in range(FEAT_TILES):
                m = j * FEAT_TILES + t
                normed = stage.tile([P, BATCH], F32, tag="f32_tile", bufs=F32_TILE_BUFS)
                nc.vector.scalar_tensor_tensor(
                    out=normed[:],
                    in0=u_tile(m),
                    scalar=hb_cols[:, m : m + 1],
                    in1=rstd[:],
                    op0=ALU.add,
                    op1=ALU.mult,
                )
                nc.scalar.activation(
                    out=h_rows[:, t, :], in_=normed[:], func=ACT.Silu, scale=hg_cols[:, m : m + 1]
                )
            if j >= 1 and G_ROWS < BATCH:
                regroup(nc.vector.tensor_copy, h_grouped[j - 1][:, G_ROWS:, :], h_rows_of[j - 1][:, :, G_ROWS:])
            for chunk in ready:
                quantise_gw(chunk)
            ready = []
            for chunk, half, bank in banks:
                nc.scalar.copy(
                    out=gw_grouped[chunk][:, half * PIECE : (half + 1) * PIECE, :], in_=bank[:]
                )
                if half == 1:
                    ready.append(chunk)
            count = (j + 1) * rest // P2_ROUNDS - j * rest // P2_ROUNDS if j < P2_ROUNDS else 0
            if j >= 1 and count == 0:
                quantise_h(j - 1)
            for n in range(count):
                if j >= 1 and n == count - 1:
                    quantise_h(j - 1)
                share(done, P2_SPLIT)
                ready.append(done)
                done += 1
            if j == BLOCKS - 1:
                for n in range(LASTV):
                    share(done, DPB)
                    ready.append(done)
                    done += 1
            h_grouped[j] = stage.tile([P, BATCH, PACK], BF16, name="h_grouped", bufs=1, align_bytes=64)
            h_rows_of[j] = h_rows
            regroup(gpsimd_copy, h_grouped[j][:, 0:G_ROWS, :], h_rows[:, :, 0:G_ROWS])
        table(ACT.Sigmoid)

        out_view = out.rearrange(batch_major, p=P)
        gate_ps = {}
        updateT = {}
        kept = {}
        reset = {}
        update = {}
        mix = {}
        mixT = {}

        def unit_tile(name, bufs):
            return stage.tile([P, TILES_PER_UNIT, BATCH], F32, name=name, bufs=bufs)

        def gate_matmuls(unit):
            j = unit // UNITS_PER_BLOCK
            for gate in (RESET, UPDATE, CAND):
                gate_ps[unit, gate] = psum_tile([P, TILES_PER_UNIT, BATCH], F32, "mm")
                for s in range(TILES_PER_UNIT):
                    first = gate * DPB + (unit * TILES_PER_UNIT + s) * P - j * DPB
                    nc.tensor.matmul_mx(
                        out=gate_ps[unit, gate][:, s, :],
                        lhsT=gw_codes[:, j, first : first + P].bitcast(FP8X4),
                        lhsT_scale=gw_scales[:, j, first : first + P],
                        rhs=h_codes[:, j, :].bitcast(FP8X4),
                        rhs_scale=h_scales[:, j, :],
                        start=True,
                        stop=True,
                    )

        def transpose_units(source, target):
            for s in range(TILES_PER_UNIT):
                for bt in range(BATCH_TILES):
                    nc.tensor.transpose(
                        target[:, bt, s * P : (s + 1) * P],
                        source[:, s, bt * P : (bt + 1) * P],
                        ident_f32[:],
                    )

        def transpose_update(unit):
            updateT[unit] = psum_tile([P, BATCH_TILES, UNIT_COLS], F32, "inT")
            transpose_units(update[unit], updateT[unit])

        def transpose_mix(unit, tag):
            mixT[unit] = psum_tile([P, BATCH_TILES, UNIT_COLS], F32, tag)
            transpose_units(mix[unit], mixT[unit])

        def gate_bias(unit, gate, s):
            j, t = divmod(unit * TILES_PER_UNIT + s, FEAT_TILES)
            return gb_cols[:, j, gate, t : t + 1]

        def sigmoids(unit):
            reset[unit] = unit_tile("reset", STAGE_BUFS)
            update[unit] = unit_tile("update", STEPS_ALIVE)
            for gate, result in ((RESET, reset[unit]), (UPDATE, update[unit])):
                for s in range(TILES_PER_UNIT):
                    nc.scalar.activation(
                        out=result[:, s, :],
                        in_=gate_ps[unit, gate][:, s, :],
                        func=ACT.Sigmoid,
                        bias=gate_bias(unit, gate, s),
                    )

        def reset_candidate(unit):
            mix[unit] = unit_tile("mix", STEPS_ALIVE)
            for s in range(TILES_PER_UNIT):
                nc.vector.scalar_tensor_tensor(
                    out=mix[unit][:, s, :],
                    in0=gate_ps[unit, CAND][:, s, :],
                    scalar=gate_bias(unit, CAND, s),
                    in1=reset[unit][:, s, :],
                    op0=ALU.add,
                    op1=ALU.mult,
                )

        def candidate(unit):
            nc.scalar.activation(out=mix[unit][:], in_=mix[unit][:], func=ACT.Tanh)

        def apply_update(unit, multiplier):
            multiplier.tensor_tensor(
                out=mix[unit][:], in0=mix[unit][:], in1=update[unit][:], op=ALU.mult
            )

        def unit_cols(unit):
            return slice(unit * UNIT_COLS, (unit + 1) * UNIT_COLS)

        def keep_state(unit):
            kept[unit] = stage.tile([P, BATCH_TILES, UNIT_COLS], F32, name="kept", bufs=KEPT_BUFS)
            nc.vector.scalar_tensor_tensor(
                out=kept[unit][:],
                in0=updateT[unit][:],
                scalar=1.0,
                in1=deter_sb[:, :, unit_cols(unit)],
                op0=ALU.subtract,
                op1=ALU.mult,
            )

        def finish(unit):
            new_state = stage.tile([P, BATCH_TILES, UNIT_COLS], F32, bufs=STORE_BUFS)
            nc.vector.tensor_tensor(
                out=new_state[:], in0=mixT[unit][:], in1=kept[unit][:], op=ALU.subtract
            )
            nc.sync.dma_start(out=out_view[:, :, unit_cols(unit)], in_=new_state[:])

        gate_matmuls(0)
        for step in range(UNITS):
            sigmoids(step)
            if step + 1 < UNITS:
                gate_matmuls(step + 1)
            transpose_update(step)
            if step >= 1:
                candidate(step - 1)
            reset_candidate(step)
            if step >= 3:
                finish(step - 3)
            if step >= 2:
                transpose_mix(step - 2, "outT")
            if step == 0:
                for chunk in ready:
                    quantise_gw(chunk)
            if step == 0 and G_ROWS < BATCH:
                regroup(nc.vector.tensor_copy, h_grouped[BLOCKS - 1][:, G_ROWS:, :], h_rows_of[BLOCKS - 1][:, :, G_ROWS:])
            if step == H_STEP:
                quantise_h(BLOCKS - 1)
            if G_CHUNKS and step >= 0:
                piece = step - 1
                chunk = CHUNKS - G_CHUNKS + piece // G_PIECES
                if piece >= 0 and chunk < CHUNKS:
                    w = DPB // G_PIECES
                    q = piece % G_PIECES
                    regroup_gw(gpsimd_copy, chunk, q * w, q * w + w)
                if piece > 0 and piece % G_PIECES == 0 and chunk <= CHUNKS:
                    quantise_gw(chunk - 1)
            if step >= 1:
                keep_state(step - 1)
                apply_update(step - 1, nc.gpsimd)

        last = UNITS - 1
        keep_state(last)
        finish(last - 2)
        for s in range(TILES_PER_UNIT):
            nc.scalar.activation(out=mix[last][:, s, :], in_=mix[last][:, s, :], func=ACT.Tanh)
        for s in range(TILES_PER_UNIT):
            nc.vector.tensor_tensor(
                out=mix[last][:, s, :], in0=mix[last][:, s, :], in1=update[last][:, s, :], op=ALU.mult
            )
        transpose_mix(last - 1, "mm")
        halves = []
        for s in range(TILES_PER_UNIT):
            half = psum_tile([P, BATCH_TILES, P], F32, "mm")
            for bt in range(BATCH_TILES):
                nc.tensor.transpose(
                    half[:, bt, :], mix[last][:, s, bt * P : (bt + 1) * P], ident_f32[:]
                )
            halves.append(half)
        finish(last - 1)
        for s in range(TILES_PER_UNIT):
            new_half = stage.tile([P, BATCH_TILES, P], F32, tag="f32_tile", bufs=F32_TILE_BUFS)
            nc.vector.tensor_tensor(
                out=new_half[:],
                in0=halves[s][:],
                in1=kept[last][:, :, s * P : (s + 1) * P],
                op=ALU.subtract,
            )
            first = last * UNIT_COLS + s * P
            nc.sync.dma_start(out=out_view[:, :, first : first + P], in_=new_half[:])
